import numpy as np
import ml_dtypes


def mxq(x, axis, fmt="e4m3"):
    dtype, down = {"e4m3": (ml_dtypes.float8_e4m3fn, 7), "e5m2": (ml_dtypes.float8_e5m2, 14)}[fmt]
    v = np.moveaxis(np.asarray(x, np.float32).astype(ml_dtypes.bfloat16).astype(np.float64), axis, -1)
    blocks = v.reshape(v.shape[:-1] + (-1, 32))
    amax = np.abs(blocks).max(-1, keepdims=True)
    byte = np.maximum(np.where(amax > 0, np.frexp(amax)[1] - 1 + 127, 0) - down, 1)
    scale = np.exp2(byte - 127.0)
    codes = (blocks / scale).astype(np.float32).astype(dtype).astype(np.float64)
    return np.moveaxis((codes * scale).reshape(v.shape), -1, axis)


WIDE = False


def mx_kscale(k):
    if not WIDE:
        return np.ones(k)
    levels = np.array([10, -10, 5, -5, 0])
    if k % 512:
        return np.exp2(np.random.permutation(np.resize(levels, k // 32))).repeat(32)
    a = np.empty((k // 512, 16))
    for p in range(k // 512):
        a[p, :8] = np.random.permutation(np.resize(levels, 8))
        for g in range(8):
            far = levels[np.abs(levels - a[p, g]) >= 10]
            a[p, g + 8] = far[np.random.randint(len(far))]
    return np.exp2(a.ravel()).repeat(32)


BF16 = ml_dtypes.bfloat16


def bf(x):
    return np.asarray(x, np.float32).astype(BF16)


def f64(x):
    return np.asarray(x).astype(np.float64)


T, B, D, H, L = 32, 128, 1024, 256, 1
G = 4


def sigmoid(v):
    return 1.0 / (1.0 + np.exp(-v))


def setup_inputs():
    s = mx_kscale(D)
    W = np.random.standard_normal((L, G, D + H, H)) * 1.5 / np.sqrt(D + H)
    W[0, :, :D, :] /= s[:, None]
    return {"inputs": bf(np.random.standard_normal((T, B, D)) * s),
            "h_0": bf(np.random.standard_normal((L, B, H)) * 0.5),
            "c_0": bf(np.random.standard_normal((L, B, H))),
            "W": bf(W),
            "b": bf(np.random.standard_normal((L, G, H)) * 0.3)}


def reference(inputs, h_0, c_0, W, b):
    x = f64(inputs)
    h_0, c_0, W, b = f64(h_0), f64(c_0), f64(W), f64(b)
    h_layers, c_layers = [], []
    for l in range(L):
        wx = W[l][:, :D, :].transpose(1, 0, 2).reshape(D, G * H)
        wh = W[l][:, D:, :].transpose(1, 0, 2).reshape(H, G * H)
        xin = x if l == 0 else x
        gx = (mxq(xin.reshape(T * B, D), 1, "e4m3") @ mxq(wx, 0, "e4m3")).reshape(T, B, G, H)
        gh = (h_0[l] @ wh).reshape(B, G, H)
        gates = gx + gh + b[l]
        f = sigmoid(gates[..., 0, :])
        i = sigmoid(gates[..., 1, :])
        g = np.tanh(gates[..., 2, :])
        o = sigmoid(gates[..., 3, :])
        c = f * c_0[l] + i * g
        h = o * np.tanh(c)
        x = h
        h_layers.append(h)
        c_layers.append(c)
    h_n = np.stack(h_layers, axis=1)
    c_n = np.stack(c_layers, axis=1)
    return x, np.stack([h_n, c_n], axis=0)

@@ -1,0 +1,260 @@
+from contextlib import ExitStack
+
+import concourse.mybir as mybir
+from concourse.masks import make_identity
+
+F32 = mybir.dt.float32
+BF16 = mybir.dt.bfloat16
+U32 = mybir.dt.uint32
+U8 = mybir.dt.uint8
+FP8X4 = mybir.dt.float8_e4m3fn_x4
+SIGMOID = mybir.ActivationFunctionType.Sigmoid
+TANH = mybir.ActivationFunctionType.Tanh
+ADD = mybir.AluOpType.add
+MULT = mybir.AluOpType.mult
+
+T, B, D, H, GATES = 32, 128, 1024, 256, 4
+P = 128
+PACK = 4
+K_PASS = P * PACK
+PASSES = D // K_PASS
+GATE_COLS = GATES * H
+BANK = 512
+HALVES = GATE_COLS // BANK
+GATES_PER_HALF = GATES // HALVES
+SUBS = 2
+ROUNDS = T // SUBS
+WORDS = D // 2
+X_BUFS = 6
+CG_BUFS = 2
+PINNED_FROM = 2
+
+FLOPS = 2 * T * B * D * GATE_COLS + 2 * B * H * GATE_COLS
+
+
+def tile_qlstm_t_kernel(tc, inputs, h_0, c_0, W, b, out_0, out_1):
+    nc = tc.nc
+    hc_steps = out_1.rearrange("a t l n h -> a (t l) n h")
+
+    with ExitStack() as stack:
+        const = stack.enter_context(tc.tile_pool(name="const", bufs=1))
+        x_pool = stack.enter_context(tc.tile_pool(name="x_pool", bufs=X_BUFS))
+        work = stack.enter_context(tc.tile_pool(name="work", bufs=3))
+        late = stack.enter_context(tc.tile_pool(name="late", bufs=4))
+        psum_t = stack.enter_context(tc.psum_pool(name="psum_t", bufs=2))
+        psum_g = stack.enter_context(tc.psum_pool(name="psum_g", bufs=6))
+
+        ident = const.tile([P, P], F32)
+        ones = const.tile([P, P], BF16)
+        b_row = const.tile([P, GATE_COLS], BF16)
+        w_raw = const.tile([P, PASSES * GATES, PACK * H], BF16)
+        w_grouped = const.tile([P, PASSES * GATES, H * PACK], BF16, align_bytes=64)
+        w_codes = const.tile([P, PASSES, GATE_COLS], U32, align_bytes=64)
+        w_scales = const.tile([P, PASSES, GATE_COLS], U8, align_bytes=64)
+        wh = const.tile([P, 2, GATE_COLS], BF16)
+        h0_sb = const.tile([P, H], BF16)
+        h0_t = const.tile([P, 2, P], BF16)
+        c0_sb = const.tile([P, H], BF16)
+        cg_bufs = [const.tile([P, SUBS, 2 * H], F32, name="cg%d" % n) for n in range(CG_BUFS)]
+        state_term = const.tile([P, GATE_COLS], F32)
+        zero_col = const.tile([P, 1], F32)
+        table_warm = const.tile([P, 1], F32)
+
+        x_tiles, xt_tiles, xg_tiles, code_tiles, scale_tiles = {}, {}, {}, {}, {}
+        acc_tiles, pre_tiles, act_tiles, fc_ig_tiles, hc_tiles, tanh_c_tiles = {}, {}, {}, {}, {}, {}
+
+        def load_x(j):
+            x_sb = x_pool.tile([P, SUBS, D], BF16)
+            nc.sync.dma_start(out=x_sb[:], in_=inputs[j * SUBS : (j + 1) * SUBS].rearrange("r p k -> p r k"))
+            x_tiles[j] = x_sb
+
+        def load_w_piece(g, j):
+            rows = W[0, j, g * K_PASS : (g + 1) * K_PASS, :]
+            nc.sync.dma_start(
+                out=w_raw[:, g * GATES + j, :],
+                in_=rows.rearrange("(q t) c -> q (t c)", t=PACK),
+            )
+
+        def load_w_half(half):
+            for g in range(PASSES):
+                for j in range(half * GATES_PER_HALF, (half + 1) * GATES_PER_HALF):
+                    load_w_piece(g, j)
+
+        nc.vector.memset(b_row[:], 0.0)
+        nc.vector.memset(ones[:], 1.0)
+        nc.vector.memset(zero_col[:], 0.0)
+        make_identity(nc, ident[:])
+        nc.scalar.activation(out=table_warm[:], in_=zero_col[:], func=SIGMOID)
+
+        load_w_half(0)
+        load_x(0)
+        nc.sync.dma_start(out=h0_sb[:], in_=h_0[0])
+        nc.sync.dma_start(out=b_row[0:1, :], in_=b.rearrange("l j c -> l (j c)"))
+        nc.sync.dma_start(out=c0_sb[:], in_=c_0[0])
+        for e in range(2):
+            nc.sync.dma_start(
+                out=wh[:, e, :].rearrange("q (j c) -> q j c", j=GATES),
+                in_=W[0, :, D : D + H, :].rearrange("j (q e) c -> q e j c", e=2)[:, e],
+            )
+        load_x(1)
+        load_w_half(1)
+        for j in range(2, X_BUFS):
+            load_x(j)
+
+        def regroup_views(g, j):
+            piece = g * GATES + j
+            src = w_raw[:, piece, :].rearrange("q (t c i) -> q c t i", t=PACK, i=4)
+            dst = w_grouped[:, piece, :].rearrange("q (c i t) -> q c t i", i=4, t=PACK)
+            return dst, src
+
+        def prepare_w_half(half):
+            first = half * GATES_PER_HALF
+            cols = slice(half * BANK, (half + 1) * BANK)
+            for g in range(PASSES):
+                dst, src = regroup_views(g, first)
+                nc.scalar.copy(out=dst, in_=src)
+                dst, src = regroup_views(g, first + 1)
+                nc.vector.tensor_copy(out=dst, in_=src)
+                piece = g * GATES + first
+                nc.vector.quantize_mx(
+                    out=w_codes[:, g, cols].bitcast(FP8X4),
+                    scales=w_scales[:, g, cols],
+                    in_=w_grouped[:, piece : piece + GATES_PER_HALF, :].rearrange("q a n -> q (a n)"),
+                )
+
+        prepare_w_half(0)
+
+        h0_ps = psum_t.tile([P, WORDS // P, P], F32, name="xt")
+        nc.tensor.transpose(out=h0_ps[:, 0, :], in_=h0_sb[:].bitcast(F32), identity=ident[:])
+        nc.vector.tensor_copy(out=h0_t[:], in_=h0_ps[:, 0, :].bitcast(BF16).rearrange("q (m e) -> q e m", e=2))
+        for half in range(HALVES):
+            cols = slice(half * BANK, (half + 1) * BANK)
+            acc = psum_g.tile([P, BANK], F32, name="acc")
+            nc.tensor.matmul(out=acc[:], lhsT=h0_t[:, 0, :], rhs=wh[:, 0, cols], start=True, stop=False)
+            nc.tensor.matmul(out=acc[:], lhsT=h0_t[:, 1, :], rhs=wh[:, 1, cols], start=False, stop=False)
+            nc.tensor.matmul(out=acc[:], lhsT=ones[:], rhs=b_row[:, cols], start=False, stop=True)
+            if half == 0:
+                nc.vector.tensor_copy(out=state_term[:, cols], in_=acc[:])
+            else:
+                nc.scalar.copy(out=state_term[:, cols], in_=acc[:])
+
+        prepare_w_half(1)
+        for cg in cg_bufs:
+            nc.vector.tensor_copy(out=cg[:, :, 0:H], in_=c0_sb[:].unsqueeze(1).to_broadcast([P, SUBS, H]))
+
+        def transpose_x(j):
+            for r in range(SUBS):
+                xt = psum_t.tile([P, WORDS // P, P], F32, name="xt")
+                x_words = x_tiles[j][:, r, :].bitcast(F32)
+                for c in range(WORDS // P):
+                    first = c // 2 * 2 * P + c % 2
+                    nc.tensor.transpose(
+                        out=xt[:, c, :], in_=x_words[:, first : first + 2 * P - 1 : 2], identity=ident[:]
+                    )
+                xt_tiles[j, r] = xt
+
+        def copy_x(j):
+            xg = work.tile([P, SUBS, D], BF16, align_bytes=64)
+            for r in range(SUBS):
+                nc.scalar.copy(
+                    out=xg[:, r, :].bitcast(F32).rearrange("q (g m u) -> q g m u", g=PASSES, u=2),
+                    in_=xt_tiles[j, r][:].rearrange("q (g u) m -> q g m u", u=2),
+                )
+            xg_tiles[j] = xg
+
+        def quantise_x(j):
+            x_codes = work.tile([P, SUBS * PASSES * P], U32, align_bytes=64)
+            x_scales = work.tile([P, SUBS * PASSES * P], U8, align_bytes=64)
+            nc.vector.quantize_mx(
+                out=x_codes[:].bitcast(FP8X4),
+                scales=x_scales[:],
+                in_=xg_tiles[j][:].rearrange("q r n -> q (r n)"),
+            )
+            code_tiles[j], scale_tiles[j] = x_codes, x_scales
+
+        def gate_matmuls(j):
+            for half in range(HALVES):
+                for r in range(SUBS):
+                    acc = psum_g.tile([P, BANK], F32, name="acc")
+                    for g in range(PASSES):
+                        m_cols = slice((r * PASSES + g) * P, (r * PASSES + g + 1) * P)
+                        n_cols = slice(half * BANK, (half + 1) * BANK)
+                        nc.tensor.matmul_mx(
+                            out=acc[:],
+                            lhsT=code_tiles[j][:, m_cols].bitcast(FP8X4),
+                            lhsT_scale=scale_tiles[j][:, m_cols],
+                            rhs=w_codes[:, g, n_cols].bitcast(FP8X4),
+                            rhs_scale=w_scales[:, g, n_cols],
+                            start=(g == 0),
+                            stop=(g == PASSES - 1),
+                        )
+                    acc_tiles[j, r, half] = acc
+
+        def add_state_term(j):
+            pre = work.tile([P, SUBS, GATE_COLS], F32)
+            for half in range(HALVES):
+                for r in range(SUBS):
+                    cols = slice(half * BANK, (half + 1) * BANK)
+                    nc.vector.tensor_tensor(
+                        out=pre[:, r, cols], in0=acc_tiles[j, r, half][:], in1=state_term[:, cols], op=ADD
+                    )
+            pre_tiles[j] = pre
+
+        def gate_functions(j):
+            pre = pre_tiles[j]
+            act = late.tile([P, SUBS, 3 * H], F32)
+            nc.scalar.activation(out=act[:, :, 0 : 2 * H], in_=pre[:, :, 0 : 2 * H], func=SIGMOID)
+            nc.scalar.activation(out=cg_bufs[j % CG_BUFS][:, :, H : 2 * H], in_=pre[:, :, 2 * H : 3 * H], func=TANH)
+            nc.scalar.activation(out=act[:, :, 2 * H : 3 * H], in_=pre[:, :, 3 * H : 4 * H], func=SIGMOID)
+            act_tiles[j] = act
+
+        def gate_products(j):
+            engine = nc.vector if j == ROUNDS - 1 else nc.gpsimd
+            fc_ig = work.tile([P, SUBS, 2 * H], F32)
+            engine.tensor_tensor(out=fc_ig[:], in0=act_tiles[j][:, :, 0 : 2 * H], in1=cg_bufs[j % CG_BUFS][:], op=MULT)
+            fc_ig_tiles[j] = fc_ig
+
+        def store(dram_steps, j, tile_rows):
+            nc.sync.dma_start(out=dram_steps[j * SUBS : (j + 1) * SUBS].rearrange("r p h -> p r h"), in_=tile_rows)
+
+        def new_c(j):
+            hc = late.tile([P, 2, SUBS, H], F32)
+            fc_ig = fc_ig_tiles[j]
+            nc.vector.tensor_tensor(out=hc[:, 1], in0=fc_ig[:, :, 0:H], in1=fc_ig[:, :, H : 2 * H], op=ADD)
+            store(hc_steps[1], j, hc[:, 1])
+            hc_tiles[j] = hc
+
+        def tanh_of_c(j):
+            tanh_c = work.tile([P, SUBS, H], F32)
+            nc.scalar.activation(out=tanh_c[:], in_=hc_tiles[j][:, 1], func=TANH)
+            tanh_c_tiles[j] = tanh_c
+
+        def new_h_and_store(j):
+            hc = hc_tiles[j]
+            o_gate = act_tiles[j][:, :, 2 * H : 3 * H]
+            nc.vector.tensor_tensor(out=hc[:, 0], in0=o_gate, in1=tanh_c_tiles[j][:], op=MULT)
+            store(hc_steps[0], j, hc[:, 0])
+            store(out_0, j, hc[:, 0])
+
+        def run(stage, j):
+            if 0 <= j < ROUNDS:
+                stage(j)
+
+        def step(i):
+            run(tanh_of_c, i - 2)
+            run(copy_x, i + 2)
+            run(gate_matmuls, i + 1)
+            run(add_state_term, i)
+            run(gate_functions, i)
+            run(gate_products, i - 1)
+            run(quantise_x, i + 2)
+            run(new_c, i - 1)
+            run(new_h_and_store, i - 2)
+            run(transpose_x, i + 3)
+            run(load_x, i + 3 + X_BUFS)
+
+        for i in range(-3, PINNED_FROM):
+            step(i)
+        with tc.manual_schedule():
+            for i in range(PINNED_FROM, ROUNDS + 2):
+                step(i)

@@ -26,8 +26,9 @@ SUBS = 2
 ROUNDS = T // SUBS
 WORDS = D // 2
 X_BUFS = 6
+EARLY = 2
 CG_BUFS = 2
-PINNED_FROM = 2
+GATE_F, GATE_I, GATE_G, GATE_O = range(GATES)
 
 FLOPS = 2 * T * B * D * GATE_COLS + 2 * B * H * GATE_COLS
 
@@ -43,6 +44,7 @@ def tile_qlstm_t_kernel(tc, inputs, h_0, c_0, W, b, out_0, out_1):
         late = stack.enter_context(tc.tile_pool(name="late", bufs=4))
         psum_t = stack.enter_context(tc.psum_pool(name="psum_t", bufs=2))
         psum_g = stack.enter_context(tc.psum_pool(name="psum_g", bufs=6))
+        stack.enter_context(tc.manual_schedule())
 
         ident = const.tile([P, P], F32)
         ones = const.tile([P, P], BF16)
@@ -65,86 +67,61 @@ def tile_qlstm_t_kernel(tc, inputs, h_0, c_0, W, b, out_0, out_1):
 
         def load_x(j):
             x_sb = x_pool.tile([P, SUBS, D], BF16)
-            nc.sync.dma_start(out=x_sb[:], in_=inputs[j * SUBS : (j + 1) * SUBS].rearrange("r p k -> p r k"))
+            if j == 0:
+                for r in range(SUBS):
+                    nc.sync.dma_start(out=x_sb[:, r, :], in_=inputs[r])
+            else:
+                nc.sync.dma_start(out=x_sb[:], in_=inputs[j * SUBS : (j + 1) * SUBS].rearrange("r p k -> p r k"))
             x_tiles[j] = x_sb
 
         def load_w_piece(g, j):
             rows = W[0, j, g * K_PASS : (g + 1) * K_PASS, :]
-            nc.sync.dma_start(
-                out=w_raw[:, g * GATES + j, :],
-                in_=rows.rearrange("(q t) c -> q (t c)", t=PACK),
-            )
+            nc.sync.dma_start(out=w_raw[:, g * GATES + j, :], in_=rows.rearrange("(q t) c -> q (t c)", t=PACK))
 
-        def load_w_half(half):
-            for g in range(PASSES):
-                for j in range(half * GATES_PER_HALF, (half + 1) * GATES_PER_HALF):
-                    load_w_piece(g, j)
-
-        nc.vector.memset(b_row[:], 0.0)
-        nc.vector.memset(ones[:], 1.0)
-        nc.vector.memset(zero_col[:], 0.0)
-        make_identity(nc, ident[:])
-        nc.scalar.activation(out=table_warm[:], in_=zero_col[:], func=SIGMOID)
-
-        load_w_half(0)
-        load_x(0)
-        nc.sync.dma_start(out=h0_sb[:], in_=h_0[0])
-        nc.sync.dma_start(out=b_row[0:1, :], in_=b.rearrange("l j c -> l (j c)"))
-        nc.sync.dma_start(out=c0_sb[:], in_=c_0[0])
-        for e in range(2):
-            nc.sync.dma_start(
-                out=wh[:, e, :].rearrange("q (j c) -> q j c", j=GATES),
-                in_=W[0, :, D : D + H, :].rearrange("j (q e) c -> q e j c", e=2)[:, e],
-            )
-        load_x(1)
-        load_w_half(1)
-        for j in range(2, X_BUFS):
-            load_x(j)
-
-        def regroup_views(g, j):
-            piece = g * GATES + j
-            src = w_raw[:, piece, :].rearrange("q (t c i) -> q c t i", t=PACK, i=4)
-            dst = w_grouped[:, piece, :].rearrange("q (c i t) -> q c t i", i=4, t=PACK)
-            return dst, src
-
-        def prepare_w_half(half):
-            first = half * GATES_PER_HALF
-            cols = slice(half * BANK, (half + 1) * BANK)
-            for g in range(PASSES):
-                dst, src = regroup_views(g, first)
-                nc.scalar.copy(out=dst, in_=src)
-                dst, src = regroup_views(g, first + 1)
-                nc.vector.tensor_copy(out=dst, in_=src)
-                piece = g * GATES + first
-                nc.vector.quantize_mx(
-                    out=w_codes[:, g, cols].bitcast(FP8X4),
-                    scales=w_scales[:, g, cols],
-                    in_=w_grouped[:, piece : piece + GATES_PER_HALF, :].rearrange("q a n -> q (a n)"),
+        def load_state_operands():
+            nc.sync.dma_start(out=h0_sb[:], in_=h_0[0])
+            nc.sync.dma_start(out=b_row[0:1, :], in_=b.rearrange("l j c -> l (j c)"))
+            for e in range(2):
+                nc.sync.dma_start(
+                    out=wh[:, e, :].rearrange("q (j c) -> q j c", j=GATES),
+                    in_=W[0, :, D : D + H, :].rearrange("j (q e) c -> q e j c", e=2)[:, e],
                 )
 
-        prepare_w_half(0)
+        def regroup_w(engine_copy, g, j):
+            piece = g * GATES + j
+            engine_copy(
+                out=w_grouped[:, piece, :].rearrange("q (c i t) -> q c t i", i=4, t=PACK),
+                in_=w_raw[:, piece, :].rearrange("q (t c i) -> q c t i", t=PACK, i=4),
+            )
 
-        h0_ps = psum_t.tile([P, WORDS // P, P], F32, name="xt")
-        nc.tensor.transpose(out=h0_ps[:, 0, :], in_=h0_sb[:].bitcast(F32), identity=ident[:])
-        nc.vector.tensor_copy(out=h0_t[:], in_=h0_ps[:, 0, :].bitcast(BF16).rearrange("q (m e) -> q e m", e=2))
-        for half in range(HALVES):
+        def quantise_w(g, half):
+            cols = slice(half * BANK, (half + 1) * BANK)
+            piece = g * GATES + half * GATES_PER_HALF
+            nc.vector.quantize_mx(
+                out=w_codes[:, g, cols].bitcast(FP8X4),
+                scales=w_scales[:, g, cols],
+                in_=w_grouped[:, piece : piece + GATES_PER_HALF, :].rearrange("q a n -> q (a n)"),
+            )
+
+        def transpose_h0():
+            h0_ps = psum_t.tile([P, WORDS // P, P], F32, name="xt")
+            nc.tensor.transpose(out=h0_ps[:, 0, :], in_=h0_sb[:].bitcast(F32), identity=ident[:])
+            nc.scalar.copy(out=h0_t[:], in_=h0_ps[:, 0, :].bitcast(BF16).rearrange("q (m e) -> q e m", e=2))
+
+        def make_state_term(half, engine_copy):
             cols = slice(half * BANK, (half + 1) * BANK)
             acc = psum_g.tile([P, BANK], F32, name="acc")
             nc.tensor.matmul(out=acc[:], lhsT=h0_t[:, 0, :], rhs=wh[:, 0, cols], start=True, stop=False)
             nc.tensor.matmul(out=acc[:], lhsT=h0_t[:, 1, :], rhs=wh[:, 1, cols], start=False, stop=False)
             nc.tensor.matmul(out=acc[:], lhsT=ones[:], rhs=b_row[:, cols], start=False, stop=True)
-            if half == 0:
-                nc.vector.tensor_copy(out=state_term[:, cols], in_=acc[:])
-            else:
-                nc.scalar.copy(out=state_term[:, cols], in_=acc[:])
-
-        prepare_w_half(1)
-        for cg in cg_bufs:
-            nc.vector.tensor_copy(out=cg[:, :, 0:H], in_=c0_sb[:].unsqueeze(1).to_broadcast([P, SUBS, H]))
+            engine_copy(out=state_term[:, cols], in_=acc[:])
 
         def transpose_x(j):
             for r in range(SUBS):
-                xt = psum_t.tile([P, WORDS // P, P], F32, name="xt")
+                if j < EARLY:
+                    xt = psum_g.tile([P, WORDS // P, P], F32, name="acc")
+                else:
+                    xt = psum_t.tile([P, WORDS // P, P], F32, name="xt")
                 x_words = x_tiles[j][:, r, :].bitcast(F32)
                 for c in range(WORDS // P):
                     first = c // 2 * 2 * P + c % 2
@@ -172,41 +149,56 @@ def tile_qlstm_t_kernel(tc, inputs, h_0, c_0, W, b, out_0, out_1):
             )
             code_tiles[j], scale_tiles[j] = x_codes, x_scales
 
+        def half_matmuls(j, half):
+            for r in range(SUBS):
+                acc = psum_g.tile([P, BANK], F32, name="acc")
+                for g in range(PASSES):
+                    m_cols = slice((r * PASSES + g) * P, (r * PASSES + g + 1) * P)
+                    n_cols = slice(half * BANK, (half + 1) * BANK)
+                    nc.tensor.matmul_mx(
+                        out=acc[:],
+                        lhsT=code_tiles[j][:, m_cols].bitcast(FP8X4),
+                        lhsT_scale=scale_tiles[j][:, m_cols],
+                        rhs=w_codes[:, g, n_cols].bitcast(FP8X4),
+                        rhs_scale=w_scales[:, g, n_cols],
+                        start=(g == 0),
+                        stop=(g == PASSES - 1),
+                    )
+                acc_tiles[j, r, half] = acc
+
         def gate_matmuls(j):
             for half in range(HALVES):
-                for r in range(SUBS):
-                    acc = psum_g.tile([P, BANK], F32, name="acc")
-                    for g in range(PASSES):
-                        m_cols = slice((r * PASSES + g) * P, (r * PASSES + g + 1) * P)
-                        n_cols = slice(half * BANK, (half + 1) * BANK)
-                        nc.tensor.matmul_mx(
-                            out=acc[:],
-                            lhsT=code_tiles[j][:, m_cols].bitcast(FP8X4),
-                            lhsT_scale=scale_tiles[j][:, m_cols],
-                            rhs=w_codes[:, g, n_cols].bitcast(FP8X4),
-                            rhs_scale=w_scales[:, g, n_cols],
-                            start=(g == 0),
-                            stop=(g == PASSES - 1),
-                        )
-                    acc_tiles[j, r, half] = acc
+                half_matmuls(j, half)
+
+        def add_state_half(j, half):
+            if half == 0:
+                pre_tiles[j] = work.tile([P, SUBS, GATE_COLS], F32, name="pre")
+            for r in range(SUBS):
+                cols = slice(half * BANK, (half + 1) * BANK)
+                nc.vector.tensor_tensor(
+                    out=pre_tiles[j][:, r, cols], in0=acc_tiles[j, r, half][:], in1=state_term[:, cols], op=ADD
+                )
 
         def add_state_term(j):
-            pre = work.tile([P, SUBS, GATE_COLS], F32)
             for half in range(HALVES):
-                for r in range(SUBS):
-                    cols = slice(half * BANK, (half + 1) * BANK)
-                    nc.vector.tensor_tensor(
-                        out=pre[:, r, cols], in0=acc_tiles[j, r, half][:], in1=state_term[:, cols], op=ADD
-                    )
-            pre_tiles[j] = pre
+                add_state_half(j, half)
+
+        def f_and_i(j):
+            act_tiles[j] = late.tile([P, SUBS, 3 * H], F32, name="act")
+            nc.scalar.activation(
+                out=act_tiles[j][:, :, 0 : 2 * H], in_=pre_tiles[j][:, :, 0 : 2 * H], func=SIGMOID
+            )
+
+        def g_and_o(j):
+            pre = pre_tiles[j]
+            nc.scalar.activation(out=cg_bufs[j % CG_BUFS][:, :, H : 2 * H], in_=pre[:, :, 2 * H : 3 * H], func=TANH)
+            nc.scalar.activation(
+                out=act_tiles[j][:, :, 2 * H : 3 * H], in_=pre[:, :, 3 * H : 4 * H], func=SIGMOID
+            )
 
         def gate_functions(j):
-            pre = pre_tiles[j]
-            act = late.tile([P, SUBS, 3 * H], F32)
-            nc.scalar.activation(out=act[:, :, 0 : 2 * H], in_=pre[:, :, 0 : 2 * H], func=SIGMOID)
-            nc.scalar.activation(out=cg_bufs[j % CG_BUFS][:, :, H : 2 * H], in_=pre[:, :, 2 * H : 3 * H], func=TANH)
-            nc.scalar.activation(out=act[:, :, 2 * H : 3 * H], in_=pre[:, :, 3 * H : 4 * H], func=SIGMOID)
-            act_tiles[j] = act
+            f_and_i(j)
+            g_and_o(j)
 
         def gate_products(j):
             engine = nc.vector if j == ROUNDS - 1 else nc.gpsimd
@@ -240,6 +232,70 @@ def tile_qlstm_t_kernel(tc, inputs, h_0, c_0, W, b, out_0, out_1):
             if 0 <= j < ROUNDS:
                 stage(j)
 
+        nc.vector.memset(zero_col[:], 0.0)
+        nc.vector.memset(b_row[:], 0.0)
+        nc.vector.memset(ones[:], 1.0)
+        make_identity(nc, ident[:])
+        nc.scalar.activation(out=table_warm[:], in_=zero_col[:], func=SIGMOID)
+        vector_copy, scalar_copy = nc.vector.tensor_copy, nc.scalar.copy
+
+        load_w_piece(0, GATE_F)
+        load_w_piece(0, GATE_I)
+        load_x(0)
+        load_w_piece(1, GATE_F)
+        load_w_piece(1, GATE_I)
+        load_state_operands()
+        load_w_piece(0, GATE_G)
+        load_w_piece(0, GATE_O)
+        load_x(1)
+        load_w_piece(1, GATE_G)
+        load_w_piece(1, GATE_O)
+        nc.sync.dma_start(out=c0_sb[:], in_=c_0[0])
+        for j in range(2, X_BUFS):
+            load_x(j)
+
+        regroup_w(vector_copy, 0, GATE_F)
+        regroup_w(vector_copy, 0, GATE_I)
+        quantise_w(0, 0)
+        transpose_x(0)
+        load_x(X_BUFS)
+        copy_x(0)
+        regroup_w(vector_copy, 1, GATE_F)
+        regroup_w(vector_copy, 1, GATE_I)
+        quantise_w(1, 0)
+        quantise_x(0)
+        transpose_h0()
+        make_state_term(0, scalar_copy)
+        make_state_term(1, scalar_copy)
+        half_matmuls(0, 0)
+        regroup_w(vector_copy, 0, GATE_G)
+        regroup_w(vector_copy, 0, GATE_O)
+        quantise_w(0, 1)
+        transpose_x(1)
+        load_x(X_BUFS + 1)
+        regroup_w(scalar_copy, 1, GATE_G)
+        copy_x(1)
+        add_state_half(0, 0)
+        regroup_w(vector_copy, 1, GATE_O)
+        quantise_w(1, 1)
+        f_and_i(0)
+        quantise_x(1)
+        transpose_x(2)
+        load_x(X_BUFS + 2)
+        half_matmuls(0, 1)
+        copy_x(2)
+        gate_matmuls(1)
+        for cg in cg_bufs:
+            for r in range(SUBS):
+                nc.gpsimd.tensor_scalar(
+                    out=cg[:, r, 0:H], in0=c0_sb[:], scalar1=1.0, scalar2=0.0, op0=MULT, op1=ADD
+                )
+        add_state_half(0, 1)
+        g_and_o(0)
+        quantise_x(2)
+        transpose_x(3)
+        load_x(X_BUFS + 3)
+
         def step(i):
             run(tanh_of_c, i - 2)
             run(copy_x, i + 2)
@@ -253,8 +309,5 @@ def tile_qlstm_t_kernel(tc, inputs, h_0, c_0, W, b, out_0, out_1):
             run(transpose_x, i + 3)
             run(load_x, i + 3 + X_BUFS)
 
-        for i in range(-3, PINNED_FROM):
+        for i in range(1, ROUNDS + 2):
             step(i)
-        with tc.manual_schedule():
-            for i in range(PINNED_FROM, ROUNDS + 2):
-                step(i)

@@ -53,7 +53,7 @@ def tile_qlstm_t_kernel(tc, inputs, h_0, c_0, W, b, out_0, out_1):
         w_grouped = const.tile([P, PASSES * GATES, H * PACK], BF16, align_bytes=64)
         w_codes = const.tile([P, PASSES, GATE_COLS], U32, align_bytes=64)
         w_scales = const.tile([P, PASSES, GATE_COLS], U8, align_bytes=64)
-        wh = const.tile([P, 2, GATE_COLS], BF16)
+        wh = const.tile([P, GATES, 2, H], BF16)
         h0_sb = const.tile([P, H], BF16)
         h0_t = const.tile([P, 2, P], BF16)
         c0_sb = const.tile([P, H], BF16)
@@ -80,12 +80,15 @@ def tile_qlstm_t_kernel(tc, inputs, h_0, c_0, W, b, out_0, out_1):
 
         def load_state_operands():
             nc.sync.dma_start(out=h0_sb[:], in_=h_0[0])
+            nc.sync.dma_start(out=c0_sb[:], in_=c_0[0])
             nc.sync.dma_start(out=b_row[0:1, :], in_=b.rearrange("l j c -> l (j c)"))
-            for e in range(2):
-                nc.sync.dma_start(
-                    out=wh[:, e, :].rearrange("q (j c) -> q j c", j=GATES),
-                    in_=W[0, :, D : D + H, :].rearrange("j (q e) c -> q e j c", e=2)[:, e],
-                )
+
+        def load_wh(half):
+            gates = slice(half * GATES_PER_HALF, (half + 1) * GATES_PER_HALF)
+            nc.sync.dma_start(
+                out=wh[:, gates].rearrange("q j e c -> q j (e c)"),
+                in_=W[0, gates, D : D + H, :].rearrange("j (q e) c -> q j (e c)", e=2),
+            )
 
         def regroup_w(engine_copy, g, j):
             piece = g * GATES + j
@@ -110,9 +113,10 @@ def tile_qlstm_t_kernel(tc, inputs, h_0, c_0, W, b, out_0, out_1):
 
         def make_state_term(half, engine_copy):
             cols = slice(half * BANK, (half + 1) * BANK)
+            gates = slice(half * GATES_PER_HALF, (half + 1) * GATES_PER_HALF)
             acc = psum_g.tile([P, BANK], F32, name="acc")
-            nc.tensor.matmul(out=acc[:], lhsT=h0_t[:, 0, :], rhs=wh[:, 0, cols], start=True, stop=False)
-            nc.tensor.matmul(out=acc[:], lhsT=h0_t[:, 1, :], rhs=wh[:, 1, cols], start=False, stop=False)
+            nc.tensor.matmul(out=acc[:], lhsT=h0_t[:, 0, :], rhs=wh[:, gates, 0, :], start=True, stop=False)
+            nc.tensor.matmul(out=acc[:], lhsT=h0_t[:, 1, :], rhs=wh[:, gates, 1, :], start=False, stop=False)
             nc.tensor.matmul(out=acc[:], lhsT=ones[:], rhs=b_row[:, cols], start=False, stop=True)
             engine_copy(out=state_term[:, cols], in_=acc[:])
 
@@ -166,9 +170,11 @@ def tile_qlstm_t_kernel(tc, inputs, h_0, c_0, W, b, out_0, out_1):
                     )
                 acc_tiles[j, r, half] = acc
 
-        def gate_matmuls(j):
-            for half in range(HALVES):
-                half_matmuls(j, half)
+        def first_matmuls(j):
+            half_matmuls(j, 0)
+
+        def second_matmuls(j):
+            half_matmuls(j, 1)
 
         def add_state_half(j, half):
             if half == 0:
@@ -201,9 +207,8 @@ def tile_qlstm_t_kernel(tc, inputs, h_0, c_0, W, b, out_0, out_1):
             g_and_o(j)
 
         def gate_products(j):
-            engine = nc.vector if j == ROUNDS - 1 else nc.gpsimd
             fc_ig = work.tile([P, SUBS, 2 * H], F32)
-            engine.tensor_tensor(out=fc_ig[:], in0=act_tiles[j][:, :, 0 : 2 * H], in1=cg_bufs[j % CG_BUFS][:], op=MULT)
+            nc.gpsimd.tensor_tensor(out=fc_ig[:], in0=act_tiles[j][:, :, 0 : 2 * H], in1=cg_bufs[j % CG_BUFS][:], op=MULT)
             fc_ig_tiles[j] = fc_ig
 
         def store(dram_steps, j, tile_rows):
@@ -233,7 +238,7 @@ def tile_qlstm_t_kernel(tc, inputs, h_0, c_0, W, b, out_0, out_1):
                 stage(j)
 
         nc.vector.memset(zero_col[:], 0.0)
-        nc.vector.memset(b_row[:], 0.0)
+        nc.vector.memset(b_row[:].bitcast(U32), 0)
         nc.vector.memset(ones[:], 1.0)
         make_identity(nc, ident[:])
         nc.scalar.activation(out=table_warm[:], in_=zero_col[:], func=SIGMOID)
@@ -245,12 +250,13 @@ def tile_qlstm_t_kernel(tc, inputs, h_0, c_0, W, b, out_0, out_1):
         load_w_piece(1, GATE_F)
         load_w_piece(1, GATE_I)
         load_state_operands()
+        load_wh(0)
         load_w_piece(0, GATE_G)
         load_w_piece(0, GATE_O)
         load_x(1)
         load_w_piece(1, GATE_G)
         load_w_piece(1, GATE_O)
-        nc.sync.dma_start(out=c0_sb[:], in_=c_0[0])
+        load_wh(1)
         for j in range(2, X_BUFS):
             load_x(j)
 
@@ -266,7 +272,8 @@ def tile_qlstm_t_kernel(tc, inputs, h_0, c_0, W, b, out_0, out_1):
         quantise_x(0)
         transpose_h0()
         make_state_term(0, scalar_copy)
-        make_state_term(1, scalar_copy)
+        for cg in cg_bufs:
+            nc.scalar.copy(out=cg[:, :, 0:H], in_=c0_sb[:].unsqueeze(1).to_broadcast([P, SUBS, H]))
         half_matmuls(0, 0)
         regroup_w(vector_copy, 0, GATE_G)
         regroup_w(vector_copy, 0, GATE_O)
@@ -278,36 +285,74 @@ def tile_qlstm_t_kernel(tc, inputs, h_0, c_0, W, b, out_0, out_1):
         add_state_half(0, 0)
         regroup_w(vector_copy, 1, GATE_O)
         quantise_w(1, 1)
+        make_state_term(1, scalar_copy)
         f_and_i(0)
         quantise_x(1)
         transpose_x(2)
         load_x(X_BUFS + 2)
         half_matmuls(0, 1)
         copy_x(2)
-        gate_matmuls(1)
-        for cg in cg_bufs:
-            for r in range(SUBS):
-                nc.gpsimd.tensor_scalar(
-                    out=cg[:, r, 0:H], in0=c0_sb[:], scalar1=1.0, scalar2=0.0, op0=MULT, op1=ADD
-                )
+        half_matmuls(1, 0)
+        transpose_x(3)
+        load_x(X_BUFS + 3)
+        half_matmuls(1, 1)
         add_state_half(0, 1)
         g_and_o(0)
         quantise_x(2)
-        transpose_x(3)
-        load_x(X_BUFS + 3)
 
         def step(i):
             run(tanh_of_c, i - 2)
             run(copy_x, i + 2)
-            run(gate_matmuls, i + 1)
+            run(first_matmuls, i + 1)
+            run(transpose_x, i + 3)
+            run(second_matmuls, i + 1)
             run(add_state_term, i)
             run(gate_functions, i)
             run(gate_products, i - 1)
             run(quantise_x, i + 2)
             run(new_c, i - 1)
             run(new_h_and_store, i - 2)
-            run(transpose_x, i + 3)
             run(load_x, i + 3 + X_BUFS)
 
-        for i in range(1, ROUNDS + 2):
+        for i in range(1, ROUNDS - 1):
             step(i)
+
+        last = ROUNDS - 1
+        cg = cg_bufs[last % CG_BUFS]
+        pre = work.tile([P, SUBS, GATE_COLS], F32)
+        act = late.tile([P, SUBS, 3 * H], F32)
+        hc = late.tile([P, 2, SUBS, H], F32)
+        fc_ig = work.tile([P, SUBS, 2 * H], F32)
+        tanh_c = work.tile([P, SUBS, H], F32)
+
+        def last_sums(r):
+            for half in range(HALVES):
+                cols = slice(half * BANK, (half + 1) * BANK)
+                nc.vector.tensor_tensor(
+                    out=pre[:, r, cols], in0=acc_tiles[last, r, half][:], in1=state_term[:, cols], op=ADD
+                )
+            nc.scalar.activation(out=act[:, r, 0 : 2 * H], in_=pre[:, r, 0 : 2 * H], func=SIGMOID)
+            nc.scalar.activation(out=cg[:, r, H : 2 * H], in_=pre[:, r, 2 * H : 3 * H], func=TANH)
+
+        def last_products(r):
+            nc.vector.tensor_tensor(out=fc_ig[:, r], in0=act[:, r, 0 : 2 * H], in1=cg[:, r], op=MULT)
+
+        tanh_of_c(last - 2)
+        gate_products(last - 1)
+        for r in range(SUBS):
+            last_sums(r)
+        new_h_and_store(last - 2)
+        new_c(last - 1)
+        for r in range(SUBS):
+            last_products(r)
+        tanh_of_c(last - 1)
+        nc.scalar.activation(out=act[:, :, 2 * H : 3 * H], in_=pre[:, :, 3 * H : 4 * H], func=SIGMOID)
+        new_h_and_store(last - 1)
+        for r in range(SUBS):
+            nc.vector.tensor_tensor(out=hc[:, 1, r], in0=fc_ig[:, r, 0:H], in1=fc_ig[:, r, H : 2 * H], op=ADD)
+            nc.scalar.activation(out=tanh_c[:, r], in_=hc[:, 1, r], func=TANH)
+            nc.sync.dma_start(out=hc_steps[1, last * SUBS + r], in_=hc[:, 1, r])
+        for r in range(SUBS):
+            nc.vector.tensor_tensor(out=hc[:, 0, r], in0=act[:, r, 2 * H : 3 * H], in1=tanh_c[:, r], op=MULT)
+            nc.sync.dma_start(out=hc_steps[0, last * SUBS + r], in_=hc[:, 0, r])
+            nc.sync.dma_start(out=out_0[last * SUBS + r], in_=hc[:, 0, r])

@@ -43,7 +43,8 @@ def tile_qlstm_t_kernel(tc, inputs, h_0, c_0, W, b, out_0, out_1):
         work = stack.enter_context(tc.tile_pool(name="work", bufs=3))
         late = stack.enter_context(tc.tile_pool(name="late", bufs=4))
         psum_t = stack.enter_context(tc.psum_pool(name="psum_t", bufs=2))
-        psum_g = stack.enter_context(tc.psum_pool(name="psum_g", bufs=6))
+        psum_c = stack.enter_context(tc.psum_pool(name="psum_c", bufs=1))
+        psum_g = stack.enter_context(tc.psum_pool(name="psum_g", bufs=5))
         stack.enter_context(tc.manual_schedule())
 
         ident = const.tile([P, P], F32)
@@ -57,13 +58,14 @@ def tile_qlstm_t_kernel(tc, inputs, h_0, c_0, W, b, out_0, out_1):
         h0_sb = const.tile([P, H], BF16)
         h0_t = const.tile([P, 2, P], BF16)
         c0_sb = const.tile([P, H], BF16)
-        cg_bufs = [const.tile([P, SUBS, 2 * H], F32, name="cg%d" % n) for n in range(CG_BUFS)]
+        ident_bf = const.tile([P, P], BF16)
+        c0_ps = psum_c.tile([P, SUBS, H], F32)
         state_term = const.tile([P, GATE_COLS], F32)
         zero_col = const.tile([P, 1], F32)
         table_warm = const.tile([P, 1], F32)
 
         x_tiles, xt_tiles, xg_tiles, code_tiles, scale_tiles = {}, {}, {}, {}, {}
-        acc_tiles, pre_tiles, act_tiles, fc_ig_tiles, hc_tiles, tanh_c_tiles = {}, {}, {}, {}, {}, {}
+        acc_tiles, pre_tiles, act_tiles, fc_tiles, ig_tiles, hc_tiles, tanh_c_tiles = {}, {}, {}, {}, {}, {}, {}
 
         def load_x(j):
             x_sb = x_pool.tile([P, SUBS, D], BF16)
@@ -190,46 +192,56 @@ def tile_qlstm_t_kernel(tc, inputs, h_0, c_0, W, b, out_0, out_1):
                 add_state_half(j, half)
 
         def f_and_i(j):
-            act_tiles[j] = late.tile([P, SUBS, 3 * H], F32, name="act")
+            act_tiles[j] = late.tile([P, SUBS, GATE_COLS], F32, name="act")
             nc.scalar.activation(
                 out=act_tiles[j][:, :, 0 : 2 * H], in_=pre_tiles[j][:, :, 0 : 2 * H], func=SIGMOID
             )
 
         def g_and_o(j):
-            pre = pre_tiles[j]
-            nc.scalar.activation(out=cg_bufs[j % CG_BUFS][:, :, H : 2 * H], in_=pre[:, :, 2 * H : 3 * H], func=TANH)
-            nc.scalar.activation(
-                out=act_tiles[j][:, :, 2 * H : 3 * H], in_=pre[:, :, 3 * H : 4 * H], func=SIGMOID
-            )
+            for gate, func in ((GATE_G, TANH), (GATE_O, SIGMOID)):
+                cols = slice(gate * H, (gate + 1) * H)
+                nc.scalar.activation(out=act_tiles[j][:, :, cols], in_=pre_tiles[j][:, :, cols], func=func)
 
         def gate_functions(j):
             f_and_i(j)
             g_and_o(j)
 
-        def gate_products(j):
-            fc_ig = work.tile([P, SUBS, 2 * H], F32)
-            nc.gpsimd.tensor_tensor(out=fc_ig[:], in0=act_tiles[j][:, :, 0 : 2 * H], in1=cg_bufs[j % CG_BUFS][:], op=MULT)
-            fc_ig_tiles[j] = fc_ig
+        def f_times_c0(j):
+            fc_tiles[j] = work.tile([P, SUBS, H], F32, name="fc")
+            nc.vector.tensor_tensor(out=fc_tiles[j][:], in0=act_tiles[j][:, :, 0:H], in1=c0_ps[:], op=MULT)
+
+        def i_times_g(j):
+            ig_tiles[j] = work.tile([P, SUBS, H], F32, name="ig")
+            nc.gpsimd.tensor_tensor(
+                out=ig_tiles[j][:], in0=act_tiles[j][:, :, H : 2 * H], in1=act_tiles[j][:, :, 2 * H : 3 * H], op=MULT
+            )
 
         def store(dram_steps, j, tile_rows):
             nc.sync.dma_start(out=dram_steps[j * SUBS : (j + 1) * SUBS].rearrange("r p h -> p r h"), in_=tile_rows)
 
-        def new_c(j):
-            hc = late.tile([P, 2, SUBS, H], F32)
-            fc_ig = fc_ig_tiles[j]
-            nc.vector.tensor_tensor(out=hc[:, 1], in0=fc_ig[:, :, 0:H], in1=fc_ig[:, :, H : 2 * H], op=ADD)
-            store(hc_steps[1], j, hc[:, 1])
-            hc_tiles[j] = hc
+        def new_c_tile(engine, j, r):
+            if j not in hc_tiles:
+                hc_tiles[j] = late.tile([P, 2, SUBS, H], F32, name="hc")
+            engine.tensor_tensor(out=hc_tiles[j][:, 1, r], in0=fc_tiles[j][:, r], in1=ig_tiles[j][:, r], op=ADD)
+
+        def c_on_gpsimd(j):
+            new_c_tile(nc.gpsimd, j, 1)
+
+        def c_on_vector(j):
+            new_c_tile(nc.vector, j, 0)
+
+        def store_c(j):
+            store(hc_steps[1], j, hc_tiles[j][:, 1])
 
         def tanh_of_c(j):
             tanh_c = work.tile([P, SUBS, H], F32)
             nc.scalar.activation(out=tanh_c[:], in_=hc_tiles[j][:, 1], func=TANH)
             tanh_c_tiles[j] = tanh_c
 
-        def new_h_and_store(j):
+        def new_h_and_store(j, engine=None):
             hc = hc_tiles[j]
-            o_gate = act_tiles[j][:, :, 2 * H : 3 * H]
-            nc.vector.tensor_tensor(out=hc[:, 0], in0=o_gate, in1=tanh_c_tiles[j][:], op=MULT)
+            o_gate = act_tiles[j][:, :, 3 * H : 4 * H]
+            (engine or nc.gpsimd).tensor_tensor(out=hc[:, 0], in0=o_gate, in1=tanh_c_tiles[j][:], op=MULT)
             store(hc_steps[0], j, hc[:, 0])
             store(out_0, j, hc[:, 0])
 
@@ -272,8 +284,9 @@ def tile_qlstm_t_kernel(tc, inputs, h_0, c_0, W, b, out_0, out_1):
         quantise_x(0)
         transpose_h0()
         make_state_term(0, scalar_copy)
-        for cg in cg_bufs:
-            nc.scalar.copy(out=cg[:, :, 0:H], in_=c0_sb[:].unsqueeze(1).to_broadcast([P, SUBS, H]))
+        nc.vector.tensor_copy(out=ident_bf[:], in_=ident[:])
+        for r in range(SUBS):
+            nc.tensor.matmul(out=c0_ps[:, r, :], lhsT=ident_bf[:], rhs=c0_sb[:], start=True, stop=True)
         half_matmuls(0, 0)
         regroup_w(vector_copy, 0, GATE_G)
         regroup_w(vector_copy, 0, GATE_O)
@@ -306,23 +319,26 @@ def tile_qlstm_t_kernel(tc, inputs, h_0, c_0, W, b, out_0, out_1):
             run(first_matmuls, i + 1)
             run(transpose_x, i + 3)
             run(second_matmuls, i + 1)
+            run(i_times_g, i - 1)
+            run(f_times_c0, i - 1)
+            run(new_h_and_store, i - 2)
+            run(c_on_gpsimd, i - 1)
             run(add_state_term, i)
             run(gate_functions, i)
-            run(gate_products, i - 1)
             run(quantise_x, i + 2)
-            run(new_c, i - 1)
-            run(new_h_and_store, i - 2)
+            run(c_on_vector, i - 1)
+            run(store_c, i - 1)
             run(load_x, i + 3 + X_BUFS)
 
         for i in range(1, ROUNDS - 1):
             step(i)
 
         last = ROUNDS - 1
-        cg = cg_bufs[last % CG_BUFS]
         pre = work.tile([P, SUBS, GATE_COLS], F32)
-        act = late.tile([P, SUBS, 3 * H], F32)
+        act = late.tile([P, SUBS, GATE_COLS], F32)
         hc = late.tile([P, 2, SUBS, H], F32)
-        fc_ig = work.tile([P, SUBS, 2 * H], F32)
+        fc = work.tile([P, SUBS, H], F32)
+        ig = work.tile([P, SUBS, H], F32)
         tanh_c = work.tile([P, SUBS, H], F32)
 
         def last_sums(r):
@@ -332,27 +348,31 @@ def tile_qlstm_t_kernel(tc, inputs, h_0, c_0, W, b, out_0, out_1):
                     out=pre[:, r, cols], in0=acc_tiles[last, r, half][:], in1=state_term[:, cols], op=ADD
                 )
             nc.scalar.activation(out=act[:, r, 0 : 2 * H], in_=pre[:, r, 0 : 2 * H], func=SIGMOID)
-            nc.scalar.activation(out=cg[:, r, H : 2 * H], in_=pre[:, r, 2 * H : 3 * H], func=TANH)
+            nc.scalar.activation(out=act[:, r, 2 * H : 3 * H], in_=pre[:, r, 2 * H : 3 * H], func=TANH)
 
-        def last_products(r):
-            nc.vector.tensor_tensor(out=fc_ig[:, r], in0=act[:, r, 0 : 2 * H], in1=cg[:, r], op=MULT)
+        def last_products(engine, r):
+            engine.tensor_tensor(out=ig[:, r], in0=act[:, r, H : 2 * H], in1=act[:, r, 2 * H : 3 * H], op=MULT)
+            nc.vector.tensor_tensor(out=fc[:, r], in0=act[:, r, 0:H], in1=c0_ps[:, r], op=MULT)
 
         tanh_of_c(last - 2)
-        gate_products(last - 1)
-        for r in range(SUBS):
-            last_sums(r)
+        i_times_g(last - 1)
+        f_times_c0(last - 1)
         new_h_and_store(last - 2)
-        new_c(last - 1)
+        last_sums(0)
+        last_sums(1)
         for r in range(SUBS):
-            last_products(r)
+            new_c_tile(nc.vector, last - 1, r)
+        store_c(last - 1)
         tanh_of_c(last - 1)
-        nc.scalar.activation(out=act[:, :, 2 * H : 3 * H], in_=pre[:, :, 3 * H : 4 * H], func=SIGMOID)
-        new_h_and_store(last - 1)
+        nc.scalar.activation(out=act[:, :, 3 * H : 4 * H], in_=pre[:, :, 3 * H : 4 * H], func=SIGMOID)
+        last_products(nc.vector, 0)
+        last_products(nc.vector, 1)
+        new_h_and_store(last - 1, nc.vector)
         for r in range(SUBS):
-            nc.vector.tensor_tensor(out=hc[:, 1, r], in0=fc_ig[:, r, 0:H], in1=fc_ig[:, r, H : 2 * H], op=ADD)
+            nc.vector.tensor_tensor(out=hc[:, 1, r], in0=fc[:, r], in1=ig[:, r], op=ADD)
             nc.scalar.activation(out=tanh_c[:, r], in_=hc[:, 1, r], func=TANH)
             nc.sync.dma_start(out=hc_steps[1, last * SUBS + r], in_=hc[:, 1, r])
         for r in range(SUBS):
-            nc.vector.tensor_tensor(out=hc[:, 0, r], in0=act[:, r, 2 * H : 3 * H], in1=tanh_c[:, r], op=MULT)
+            nc.vector.tensor_tensor(out=hc[:, 0, r], in0=act[:, r, 3 * H : 4 * H], in1=tanh_c[:, r], op=MULT)
             nc.sync.dma_start(out=hc_steps[0, last * SUBS + r], in_=hc[:, 0, r])
             nc.sync.dma_start(out=out_0[last * SUBS + r], in_=hc[:, 0, r])

@@ -228,7 +228,8 @@ def tile_qlstm_t_kernel(tc, inputs, h_0, c_0, W, b, out_0, out_1):
             new_c_tile(nc.gpsimd, j, 1)
 
         def c_on_vector(j):
-            new_c_tile(nc.vector, j, 0)
+            hc_tiles[j] = late.tile([P, 2, SUBS, H], F32, name="hc")
+            nc.vector.tensor_tensor(out=hc_tiles[j][:, 1], in0=fc_tiles[j][:], in1=ig_tiles[j][:], op=ADD)
 
         def store_c(j):
             store(hc_steps[1], j, hc_tiles[j][:, 1])
@@ -322,7 +323,6 @@ def tile_qlstm_t_kernel(tc, inputs, h_0, c_0, W, b, out_0, out_1):
             run(i_times_g, i - 1)
             run(f_times_c0, i - 1)
             run(new_h_and_store, i - 2)
-            run(c_on_gpsimd, i - 1)
             run(add_state_term, i)
             run(gate_functions, i)
             run(quantise_x, i + 2)

@@ -29,6 +29,7 @@ X_BUFS = 6
 EARLY = 2
 CG_BUFS = 2
 GATE_F, GATE_I, GATE_G, GATE_O = range(GATES)
+F_SHARE = 32
 
 FLOPS = 2 * T * B * D * GATE_COLS + 2 * B * H * GATE_COLS
 
@@ -60,12 +61,13 @@ def tile_qlstm_t_kernel(tc, inputs, h_0, c_0, W, b, out_0, out_1):
         c0_sb = const.tile([P, H], BF16)
         ident_bf = const.tile([P, P], BF16)
         c0_ps = psum_c.tile([P, SUBS, H], F32)
+        cg_bufs = [const.tile([P, SUBS, F_SHARE + H], F32, name="cg%d" % n) for n in range(CG_BUFS)]
         state_term = const.tile([P, GATE_COLS], F32)
         zero_col = const.tile([P, 1], F32)
         table_warm = const.tile([P, 1], F32)
 
         x_tiles, xt_tiles, xg_tiles, code_tiles, scale_tiles = {}, {}, {}, {}, {}
-        acc_tiles, pre_tiles, act_tiles, fc_tiles, ig_tiles, hc_tiles, tanh_c_tiles = {}, {}, {}, {}, {}, {}, {}
+        acc_tiles, pre_tiles, act_tiles, fc_ig_tiles, hc_tiles, tanh_c_tiles = {}, {}, {}, {}, {}, {}
 
         def load_x(j):
             x_sb = x_pool.tile([P, SUBS, D], BF16)
@@ -187,33 +189,44 @@ def tile_qlstm_t_kernel(tc, inputs, h_0, c_0, W, b, out_0, out_1):
                     out=pre_tiles[j][:, r, cols], in0=acc_tiles[j, r, half][:], in1=state_term[:, cols], op=ADD
                 )
 
-        def add_state_term(j):
-            for half in range(HALVES):
-                add_state_half(j, half)
+        def add_first_half(j):
+            add_state_half(j, 0)
+
+        def add_second_half(j):
+            add_state_half(j, 1)
 
         def f_and_i(j):
-            act_tiles[j] = late.tile([P, SUBS, GATE_COLS], F32, name="act")
+            act_tiles[j] = late.tile([P, SUBS, 3 * H], F32, name="act")
             nc.scalar.activation(
                 out=act_tiles[j][:, :, 0 : 2 * H], in_=pre_tiles[j][:, :, 0 : 2 * H], func=SIGMOID
             )
 
         def g_and_o(j):
-            for gate, func in ((GATE_G, TANH), (GATE_O, SIGMOID)):
-                cols = slice(gate * H, (gate + 1) * H)
-                nc.scalar.activation(out=act_tiles[j][:, :, cols], in_=pre_tiles[j][:, :, cols], func=func)
+            pre = pre_tiles[j]
+            nc.scalar.activation(
+                out=cg_bufs[j % CG_BUFS][:, :, F_SHARE:], in_=pre[:, :, 2 * H : 3 * H], func=TANH
+            )
+            nc.scalar.activation(
+                out=act_tiles[j][:, :, 2 * H : 3 * H], in_=pre[:, :, 3 * H : 4 * H], func=SIGMOID
+            )
 
         def gate_functions(j):
             f_and_i(j)
             g_and_o(j)
 
         def f_times_c0(j):
-            fc_tiles[j] = work.tile([P, SUBS, H], F32, name="fc")
-            nc.vector.tensor_tensor(out=fc_tiles[j][:], in0=act_tiles[j][:, :, 0:H], in1=c0_ps[:], op=MULT)
+            own = H - F_SHARE
+            nc.vector.tensor_tensor(
+                out=fc_ig_tiles[j][:, :, 0:own], in0=act_tiles[j][:, :, 0:own], in1=c0_ps[:, :, 0:own], op=MULT
+            )
 
         def i_times_g(j):
-            ig_tiles[j] = work.tile([P, SUBS, H], F32, name="ig")
+            fc_ig_tiles[j] = work.tile([P, SUBS, 2 * H], F32, name="fc_ig")
             nc.gpsimd.tensor_tensor(
-                out=ig_tiles[j][:], in0=act_tiles[j][:, :, H : 2 * H], in1=act_tiles[j][:, :, 2 * H : 3 * H], op=MULT
+                out=fc_ig_tiles[j][:, :, H - F_SHARE :],
+                in0=act_tiles[j][:, :, H - F_SHARE : 2 * H],
+                in1=cg_bufs[j % CG_BUFS][:],
+                op=MULT,
             )
 
         def store(dram_steps, j, tile_rows):
@@ -222,14 +235,14 @@ def tile_qlstm_t_kernel(tc, inputs, h_0, c_0, W, b, out_0, out_1):
         def new_c_tile(engine, j, r):
             if j not in hc_tiles:
                 hc_tiles[j] = late.tile([P, 2, SUBS, H], F32, name="hc")
-            engine.tensor_tensor(out=hc_tiles[j][:, 1, r], in0=fc_tiles[j][:, r], in1=ig_tiles[j][:, r], op=ADD)
+            engine.tensor_tensor(out=hc_tiles[j][:, 1, r], in0=fc_ig_tiles[j][:, r, 0:H], in1=fc_ig_tiles[j][:, r, H : 2 * H], op=ADD)
 
         def c_on_gpsimd(j):
             new_c_tile(nc.gpsimd, j, 1)
 
         def c_on_vector(j):
             hc_tiles[j] = late.tile([P, 2, SUBS, H], F32, name="hc")
-            nc.vector.tensor_tensor(out=hc_tiles[j][:, 1], in0=fc_tiles[j][:], in1=ig_tiles[j][:], op=ADD)
+            nc.vector.tensor_tensor(out=hc_tiles[j][:, 1], in0=fc_ig_tiles[j][:, :, 0:H], in1=fc_ig_tiles[j][:, :, H : 2 * H], op=ADD)
 
         def store_c(j):
             store(hc_steps[1], j, hc_tiles[j][:, 1])
@@ -241,7 +254,7 @@ def tile_qlstm_t_kernel(tc, inputs, h_0, c_0, W, b, out_0, out_1):
 
         def new_h_and_store(j, engine=None):
             hc = hc_tiles[j]
-            o_gate = act_tiles[j][:, :, 3 * H : 4 * H]
+            o_gate = act_tiles[j][:, :, 2 * H : 3 * H]
             (engine or nc.gpsimd).tensor_tensor(out=hc[:, 0], in0=o_gate, in1=tanh_c_tiles[j][:], op=MULT)
             store(hc_steps[0], j, hc[:, 0])
             store(out_0, j, hc[:, 0])
@@ -288,6 +301,10 @@ def tile_qlstm_t_kernel(tc, inputs, h_0, c_0, W, b, out_0, out_1):
         nc.vector.tensor_copy(out=ident_bf[:], in_=ident[:])
         for r in range(SUBS):
             nc.tensor.matmul(out=c0_ps[:, r, :], lhsT=ident_bf[:], rhs=c0_sb[:], start=True, stop=True)
+        for cg in cg_bufs:
+            nc.scalar.copy(
+                out=cg[:, :, 0:F_SHARE], in_=c0_sb[:, H - F_SHARE :].unsqueeze(1).to_broadcast([P, SUBS, F_SHARE])
+            )
         half_matmuls(0, 0)
         regroup_w(vector_copy, 0, GATE_G)
         regroup_w(vector_copy, 0, GATE_O)
@@ -321,9 +338,10 @@ def tile_qlstm_t_kernel(tc, inputs, h_0, c_0, W, b, out_0, out_1):
             run(transpose_x, i + 3)
             run(second_matmuls, i + 1)
             run(i_times_g, i - 1)
-            run(f_times_c0, i - 1)
             run(new_h_and_store, i - 2)
-            run(add_state_term, i)
+            run(add_first_half, i)
+            run(f_times_c0, i - 1)
+            run(add_second_half, i)
             run(gate_functions, i)
             run(quantise_x, i + 2)
             run(c_on_vector, i - 1)
@@ -335,7 +353,8 @@ def tile_qlstm_t_kernel(tc, inputs, h_0, c_0, W, b, out_0, out_1):
 
         last = ROUNDS - 1
         pre = work.tile([P, SUBS, GATE_COLS], F32)
-        act = late.tile([P, SUBS, GATE_COLS], F32)
+        act = late.tile([P, SUBS, 3 * H], F32)
+        g_gate = work.tile([P, SUBS, H], F32)
         hc = late.tile([P, 2, SUBS, H], F32)
         fc = work.tile([P, SUBS, H], F32)
         ig = work.tile([P, SUBS, H], F32)
@@ -348,10 +367,10 @@ def tile_qlstm_t_kernel(tc, inputs, h_0, c_0, W, b, out_0, out_1):
                     out=pre[:, r, cols], in0=acc_tiles[last, r, half][:], in1=state_term[:, cols], op=ADD
                 )
             nc.scalar.activation(out=act[:, r, 0 : 2 * H], in_=pre[:, r, 0 : 2 * H], func=SIGMOID)
-            nc.scalar.activation(out=act[:, r, 2 * H : 3 * H], in_=pre[:, r, 2 * H : 3 * H], func=TANH)
+            nc.scalar.activation(out=g_gate[:, r], in_=pre[:, r, 2 * H : 3 * H], func=TANH)
 
         def last_products(engine, r):
-            engine.tensor_tensor(out=ig[:, r], in0=act[:, r, H : 2 * H], in1=act[:, r, 2 * H : 3 * H], op=MULT)
+            engine.tensor_tensor(out=ig[:, r], in0=act[:, r, H : 2 * H], in1=g_gate[:, r], op=MULT)
             nc.vector.tensor_tensor(out=fc[:, r], in0=act[:, r, 0:H], in1=c0_ps[:, r], op=MULT)
 
         tanh_of_c(last - 2)
@@ -364,7 +383,7 @@ def tile_qlstm_t_kernel(tc, inputs, h_0, c_0, W, b, out_0, out_1):
             new_c_tile(nc.vector, last - 1, r)
         store_c(last - 1)
         tanh_of_c(last - 1)
-        nc.scalar.activation(out=act[:, :, 3 * H : 4 * H], in_=pre[:, :, 3 * H : 4 * H], func=SIGMOID)
+        nc.scalar.activation(out=act[:, :, 2 * H : 3 * H], in_=pre[:, :, 3 * H : 4 * H], func=SIGMOID)
         last_products(nc.vector, 0)
         last_products(nc.vector, 1)
         new_h_and_store(last - 1, nc.vector)
@@ -373,6 +392,6 @@ def tile_qlstm_t_kernel(tc, inputs, h_0, c_0, W, b, out_0, out_1):
             nc.scalar.activation(out=tanh_c[:, r], in_=hc[:, 1, r], func=TANH)
             nc.sync.dma_start(out=hc_steps[1, last * SUBS + r], in_=hc[:, 1, r])
         for r in range(SUBS):
-            nc.vector.tensor_tensor(out=hc[:, 0, r], in0=act[:, r, 3 * H : 4 * H], in1=tanh_c[:, r], op=MULT)
+            nc.vector.tensor_tensor(out=hc[:, 0, r], in0=act[:, r, 2 * H : 3 * H], in1=tanh_c[:, r], op=MULT)
             nc.sync.dma_start(out=hc_steps[0, last * SUBS + r], in_=hc[:, 0, r])
             nc.sync.dma_start(out=out_0[last * SUBS + r], in_=hc[:, 0, r])

@@ -23,6 +23,8 @@ BANK = 512
 HALVES = GATE_COLS // BANK
 GATES_PER_HALF = GATES // HALVES
 SUBS = 2
+BOTH = slice(0, SUBS)
+ONE = [slice(r, r + 1) for r in range(SUBS)]
 ROUNDS = T // SUBS
 WORDS = D // 2
 X_BUFS = 6
@@ -180,14 +182,17 @@ def tile_qlstm_t_kernel(tc, inputs, h_0, c_0, W, b, out_0, out_1):
         def second_matmuls(j):
             half_matmuls(j, 1)
 
-        def add_state_half(j, half):
-            if half == 0:
+        def add_state(j, half, r):
+            if j not in pre_tiles:
                 pre_tiles[j] = work.tile([P, SUBS, GATE_COLS], F32, name="pre")
+            cols = slice(half * BANK, (half + 1) * BANK)
+            nc.vector.tensor_tensor(
+                out=pre_tiles[j][:, r, cols], in0=acc_tiles[j, r, half][:], in1=state_term[:, cols], op=ADD
+            )
+
+        def add_state_half(j, half):
             for r in range(SUBS):
-                cols = slice(half * BANK, (half + 1) * BANK)
-                nc.vector.tensor_tensor(
-                    out=pre_tiles[j][:, r, cols], in0=acc_tiles[j, r, half][:], in1=state_term[:, cols], op=ADD
-                )
+                add_state(j, half, r)
 
         def add_first_half(j):
             add_state_half(j, 0)
@@ -195,69 +200,72 @@ def tile_qlstm_t_kernel(tc, inputs, h_0, c_0, W, b, out_0, out_1):
         def add_second_half(j):
             add_state_half(j, 1)
 
-        def f_and_i(j):
-            act_tiles[j] = late.tile([P, SUBS, 3 * H], F32, name="act")
+        def f_and_i(j, rows=BOTH):
+            if j not in act_tiles:
+                act_tiles[j] = late.tile([P, SUBS, 3 * H], F32, name="act")
             nc.scalar.activation(
-                out=act_tiles[j][:, :, 0 : 2 * H], in_=pre_tiles[j][:, :, 0 : 2 * H], func=SIGMOID
+                out=act_tiles[j][:, rows, 0 : 2 * H], in_=pre_tiles[j][:, rows, 0 : 2 * H], func=SIGMOID
+            )
+
+        def gate_g(j, rows=BOTH):
+            nc.scalar.activation(
+                out=cg_bufs[j % CG_BUFS][:, rows, F_SHARE:], in_=pre_tiles[j][:, rows, 2 * H : 3 * H], func=TANH
+            )
+
+        def gate_o(j, rows=BOTH):
+            nc.scalar.activation(
+                out=act_tiles[j][:, rows, 2 * H : 3 * H], in_=pre_tiles[j][:, rows, 3 * H : 4 * H], func=SIGMOID
             )
 
         def g_and_o(j):
-            pre = pre_tiles[j]
-            nc.scalar.activation(
-                out=cg_bufs[j % CG_BUFS][:, :, F_SHARE:], in_=pre[:, :, 2 * H : 3 * H], func=TANH
-            )
-            nc.scalar.activation(
-                out=act_tiles[j][:, :, 2 * H : 3 * H], in_=pre[:, :, 3 * H : 4 * H], func=SIGMOID
-            )
+            gate_g(j)
+            gate_o(j)
 
         def gate_functions(j):
             f_and_i(j)
             g_and_o(j)
 
-        def f_times_c0(j):
-            own = H - F_SHARE
-            nc.vector.tensor_tensor(
-                out=fc_ig_tiles[j][:, :, 0:own], in0=act_tiles[j][:, :, 0:own], in1=c0_ps[:, :, 0:own], op=MULT
-            )
-
-        def i_times_g(j):
-            fc_ig_tiles[j] = work.tile([P, SUBS, 2 * H], F32, name="fc_ig")
-            nc.gpsimd.tensor_tensor(
-                out=fc_ig_tiles[j][:, :, H - F_SHARE :],
-                in0=act_tiles[j][:, :, H - F_SHARE : 2 * H],
-                in1=cg_bufs[j % CG_BUFS][:],
+        def i_times_g(j, rows=BOTH, engine=nc.gpsimd):
+            if j not in fc_ig_tiles:
+                fc_ig_tiles[j] = work.tile([P, SUBS, 2 * H], F32, name="fc_ig")
+            engine.tensor_tensor(
+                out=fc_ig_tiles[j][:, rows, H - F_SHARE :],
+                in0=act_tiles[j][:, rows, H - F_SHARE : 2 * H],
+                in1=cg_bufs[j % CG_BUFS][:, rows],
                 op=MULT,
             )
 
-        def store(dram_steps, j, tile_rows):
-            nc.sync.dma_start(out=dram_steps[j * SUBS : (j + 1) * SUBS].rearrange("r p h -> p r h"), in_=tile_rows)
+        def f_times_c0(j, rows=BOTH):
+            own = H - F_SHARE
+            nc.vector.tensor_tensor(
+                out=fc_ig_tiles[j][:, rows, 0:own], in0=act_tiles[j][:, rows, 0:own], in1=c0_ps[:, rows, 0:own], op=MULT
+            )
 
-        def new_c_tile(engine, j, r):
+        def store(dram_steps, j, tile_rows, rows):
+            steps = slice(j * SUBS + rows.start, j * SUBS + rows.stop)
+            nc.sync.dma_start(out=dram_steps[steps].rearrange("r p h -> p r h"), in_=tile_rows)
+
+        def new_c(j, rows=BOTH):
             if j not in hc_tiles:
                 hc_tiles[j] = late.tile([P, 2, SUBS, H], F32, name="hc")
-            engine.tensor_tensor(out=hc_tiles[j][:, 1, r], in0=fc_ig_tiles[j][:, r, 0:H], in1=fc_ig_tiles[j][:, r, H : 2 * H], op=ADD)
+            c = hc_tiles[j][:, 1, rows]
+            nc.vector.tensor_tensor(
+                out=c, in0=fc_ig_tiles[j][:, rows, 0:H], in1=fc_ig_tiles[j][:, rows, H : 2 * H], op=ADD
+            )
+            store(hc_steps[1], j, c, rows)
 
-        def c_on_gpsimd(j):
-            new_c_tile(nc.gpsimd, j, 1)
+        def tanh_of_c(j, rows=BOTH):
+            if j not in tanh_c_tiles:
+                tanh_c_tiles[j] = work.tile([P, SUBS, H], F32, name="tanh_c")
+            nc.scalar.activation(out=tanh_c_tiles[j][:, rows], in_=hc_tiles[j][:, 1, rows], func=TANH)
 
-        def c_on_vector(j):
-            hc_tiles[j] = late.tile([P, 2, SUBS, H], F32, name="hc")
-            nc.vector.tensor_tensor(out=hc_tiles[j][:, 1], in0=fc_ig_tiles[j][:, :, 0:H], in1=fc_ig_tiles[j][:, :, H : 2 * H], op=ADD)
-
-        def store_c(j):
-            store(hc_steps[1], j, hc_tiles[j][:, 1])
-
-        def tanh_of_c(j):
-            tanh_c = work.tile([P, SUBS, H], F32)
-            nc.scalar.activation(out=tanh_c[:], in_=hc_tiles[j][:, 1], func=TANH)
-            tanh_c_tiles[j] = tanh_c
-
-        def new_h_and_store(j, engine=None):
-            hc = hc_tiles[j]
-            o_gate = act_tiles[j][:, :, 2 * H : 3 * H]
-            (engine or nc.gpsimd).tensor_tensor(out=hc[:, 0], in0=o_gate, in1=tanh_c_tiles[j][:], op=MULT)
-            store(hc_steps[0], j, hc[:, 0])
-            store(out_0, j, hc[:, 0])
+        def new_h(j, rows=BOTH, engine=nc.gpsimd):
+            h = hc_tiles[j][:, 0, rows]
+            engine.tensor_tensor(
+                out=h, in0=act_tiles[j][:, rows, 2 * H : 3 * H], in1=tanh_c_tiles[j][:, rows], op=MULT
+            )
+            store(hc_steps[0], j, h, rows)
+            store(out_0, j, h, rows)
 
         def run(stage, j):
             if 0 <= j < ROUNDS:
@@ -338,60 +346,52 @@ def tile_qlstm_t_kernel(tc, inputs, h_0, c_0, W, b, out_0, out_1):
             run(transpose_x, i + 3)
             run(second_matmuls, i + 1)
             run(i_times_g, i - 1)
-            run(new_h_and_store, i - 2)
+            run(new_h, i - 2)
             run(add_first_half, i)
             run(f_times_c0, i - 1)
             run(add_second_half, i)
             run(gate_functions, i)
             run(quantise_x, i + 2)
-            run(c_on_vector, i - 1)
-            run(store_c, i - 1)
+            run(new_c, i - 1)
             run(load_x, i + 3 + X_BUFS)
 
-        for i in range(1, ROUNDS - 1):
+        for i in range(1, ROUNDS - 2):
             step(i)
 
         last = ROUNDS - 1
-        pre = work.tile([P, SUBS, GATE_COLS], F32)
-        act = late.tile([P, SUBS, 3 * H], F32)
-        g_gate = work.tile([P, SUBS, H], F32)
-        hc = late.tile([P, 2, SUBS, H], F32)
-        fc = work.tile([P, SUBS, H], F32)
-        ig = work.tile([P, SUBS, H], F32)
-        tanh_c = work.tile([P, SUBS, H], F32)
-
-        def last_sums(r):
-            for half in range(HALVES):
-                cols = slice(half * BANK, (half + 1) * BANK)
-                nc.vector.tensor_tensor(
-                    out=pre[:, r, cols], in0=acc_tiles[last, r, half][:], in1=state_term[:, cols], op=ADD
-                )
-            nc.scalar.activation(out=act[:, r, 0 : 2 * H], in_=pre[:, r, 0 : 2 * H], func=SIGMOID)
-            nc.scalar.activation(out=g_gate[:, r], in_=pre[:, r, 2 * H : 3 * H], func=TANH)
-
-        def last_products(engine, r):
-            engine.tensor_tensor(out=ig[:, r], in0=act[:, r, H : 2 * H], in1=g_gate[:, r], op=MULT)
-            nc.vector.tensor_tensor(out=fc[:, r], in0=act[:, r, 0:H], in1=c0_ps[:, r], op=MULT)
-
-        tanh_of_c(last - 2)
-        i_times_g(last - 1)
-        f_times_c0(last - 1)
-        new_h_and_store(last - 2)
-        last_sums(0)
-        last_sums(1)
+        prev = last - 1
+        tanh_of_c(prev - 2)
+        first_matmuls(last)
+        second_matmuls(last)
+        i_times_g(prev - 1)
+        new_h(prev - 2)
+        add_first_half(prev)
+        f_times_c0(prev - 1)
+        add_second_half(prev)
+        f_and_i(prev)
+        gate_g(prev)
+        new_c(prev - 1)
+        tanh_of_c(prev - 1)
+        gate_o(prev)
+        i_times_g(prev, ONE[0])
+        new_h(prev - 1)
+        i_times_g(prev, ONE[1])
+        f_times_c0(prev)
         for r in range(SUBS):
-            new_c_tile(nc.vector, last - 1, r)
-        store_c(last - 1)
-        tanh_of_c(last - 1)
-        nc.scalar.activation(out=act[:, :, 2 * H : 3 * H], in_=pre[:, :, 3 * H : 4 * H], func=SIGMOID)
-        last_products(nc.vector, 0)
-        last_products(nc.vector, 1)
-        new_h_and_store(last - 1, nc.vector)
+            add_state(last, 0, r)
+            add_state(last, 1, r)
+            f_and_i(last, ONE[r])
+            gate_g(last, ONE[r])
         for r in range(SUBS):
-            nc.vector.tensor_tensor(out=hc[:, 1, r], in0=fc[:, r], in1=ig[:, r], op=ADD)
-            nc.scalar.activation(out=tanh_c[:, r], in_=hc[:, 1, r], func=TANH)
-            nc.sync.dma_start(out=hc_steps[1, last * SUBS + r], in_=hc[:, 1, r])
+            new_c(prev, ONE[r])
+            tanh_of_c(prev, ONE[r])
+        gate_o(last)
         for r in range(SUBS):
-            nc.vector.tensor_tensor(out=hc[:, 0, r], in0=act[:, r, 2 * H : 3 * H], in1=tanh_c[:, r], op=MULT)
-            nc.sync.dma_start(out=hc_steps[0, last * SUBS + r], in_=hc[:, 0, r])
-            nc.sync.dma_start(out=out_0[last * SUBS + r], in_=hc[:, 0, r])
+            i_times_g(last, ONE[r], nc.vector)
+            new_h(prev, ONE[r], nc.vector)
+            f_times_c0(last, ONE[r])
+        for r in range(SUBS):
+            new_c(last, ONE[r])
+            tanh_of_c(last, ONE[r])
+        for r in range(SUBS):
+            new_h(last, ONE[r], nc.vector)

@@ -55,8 +55,8 @@ def tile_qlstm_t_kernel(tc, inputs, h_0, c_0, W, b, out_0, out_1):
         b_row = const.tile([P, GATE_COLS], BF16)
         w_raw = const.tile([P, PASSES * GATES, PACK * H], BF16)
         w_grouped = const.tile([P, PASSES * GATES, H * PACK], BF16, align_bytes=64)
-        w_codes = const.tile([P, PASSES, GATE_COLS], U32, align_bytes=64)
-        w_scales = const.tile([P, PASSES, GATE_COLS], U8, align_bytes=64)
+        w_codes = const.tile([P, PASSES, GATE_COLS], U32, align_bytes=256)
+        w_scales = const.tile([P, PASSES, GATE_COLS], U8, align_bytes=256)
         wh = const.tile([P, GATES, 2, H], BF16)
         h0_sb = const.tile([P, H], BF16)
         h0_t = const.tile([P, 2, P], BF16)
@@ -150,8 +150,8 @@ def tile_qlstm_t_kernel(tc, inputs, h_0, c_0, W, b, out_0, out_1):
             xg_tiles[j] = xg
 
         def quantise_x(j):
-            x_codes = work.tile([P, SUBS * PASSES * P], U32, align_bytes=64)
-            x_scales = work.tile([P, SUBS * PASSES * P], U8, align_bytes=64)
+            x_codes = work.tile([P, SUBS * PASSES * P], U32, align_bytes=256)
+            x_scales = work.tile([P, SUBS * PASSES * P], U8, align_bytes=256)
             nc.vector.quantize_mx(
                 out=x_codes[:].bitcast(FP8X4),
                 scales=x_scales[:],

@@ -71,6 +71,11 @@ def tile_qlstm_t_kernel(tc, inputs, h_0, c_0, W, b, out_0, out_1):
         x_tiles, xt_tiles, xg_tiles, code_tiles, scale_tiles = {}, {}, {}, {}, {}
         acc_tiles, pre_tiles, act_tiles, fc_ig_tiles, hc_tiles, tanh_c_tiles = {}, {}, {}, {}, {}, {}
 
+        def load_x_tiles(j):
+            x_tiles[j] = x_pool.tile([P, SUBS, D], BF16, name="x_sb")
+            for r in range(SUBS):
+                nc.sync.dma_start(out=x_tiles[j][:, r, :], in_=inputs[j * SUBS + r])
+
         def load_x(j):
             x_sb = x_pool.tile([P, SUBS, D], BF16)
             if j == 0:
@@ -121,9 +126,9 @@ def tile_qlstm_t_kernel(tc, inputs, h_0, c_0, W, b, out_0, out_1):
             cols = slice(half * BANK, (half + 1) * BANK)
             gates = slice(half * GATES_PER_HALF, (half + 1) * GATES_PER_HALF)
             acc = psum_g.tile([P, BANK], F32, name="acc")
-            nc.tensor.matmul(out=acc[:], lhsT=h0_t[:, 0, :], rhs=wh[:, gates, 0, :], start=True, stop=False)
-            nc.tensor.matmul(out=acc[:], lhsT=h0_t[:, 1, :], rhs=wh[:, gates, 1, :], start=False, stop=False)
-            nc.tensor.matmul(out=acc[:], lhsT=ones[:], rhs=b_row[:, cols], start=False, stop=True)
+            nc.tensor.matmul(out=acc[:], lhsT=ones[:], rhs=b_row[:, cols], start=True, stop=False)
+            nc.tensor.matmul(out=acc[:], lhsT=h0_t[:, 0, :], rhs=wh[:, gates, 0, :], start=False, stop=False)
+            nc.tensor.matmul(out=acc[:], lhsT=h0_t[:, 1, :], rhs=wh[:, gates, 1, :], start=False, stop=True)
             engine_copy(out=state_term[:, cols], in_=acc[:])
 
         def transpose_x(j):
@@ -291,7 +296,8 @@ def tile_qlstm_t_kernel(tc, inputs, h_0, c_0, W, b, out_0, out_1):
         load_w_piece(1, GATE_G)
         load_w_piece(1, GATE_O)
         load_wh(1)
-        for j in range(2, X_BUFS):
+        load_x_tiles(2)
+        for j in range(3, X_BUFS):
             load_x(j)
 
         regroup_w(vector_copy, 0, GATE_F)

@@ -381,22 +381,22 @@ def tile_qlstm_t_kernel(tc, inputs, h_0, c_0, W, b, out_0, out_1):
         gate_o(prev)
         i_times_g(prev, ONE[0])
         new_h(prev - 1)
-        i_times_g(prev, ONE[1])
         f_times_c0(prev)
         for r in range(SUBS):
             add_state(last, 0, r)
             add_state(last, 1, r)
             f_and_i(last, ONE[r])
             gate_g(last, ONE[r])
-        for r in range(SUBS):
-            new_c(prev, ONE[r])
-            tanh_of_c(prev, ONE[r])
+        new_c(prev, ONE[0])
+        tanh_of_c(prev, ONE[0])
+        i_times_g(prev, ONE[1], nc.vector)
+        new_c(prev, ONE[1])
+        tanh_of_c(prev, ONE[1])
         gate_o(last)
         for r in range(SUBS):
             i_times_g(last, ONE[r], nc.vector)
-            new_h(prev, ONE[r], nc.vector)
             f_times_c0(last, ONE[r])
-        for r in range(SUBS):
+            new_h(prev, ONE[r], nc.vector)
             new_c(last, ONE[r])
             tanh_of_c(last, ONE[r])
         for r in range(SUBS):

from contextlib import ExitStack

import concourse.mybir as mybir
from concourse.masks import make_identity

F32 = mybir.dt.float32
BF16 = mybir.dt.bfloat16
U32 = mybir.dt.uint32
U8 = mybir.dt.uint8
FP8X4 = mybir.dt.float8_e4m3fn_x4
SIGMOID = mybir.ActivationFunctionType.Sigmoid
TANH = mybir.ActivationFunctionType.Tanh
ADD = mybir.AluOpType.add
MULT = mybir.AluOpType.mult

T, B, D, H, GATES = 32, 128, 1024, 256, 4
P = 128
PACK = 4
K_PASS = P * PACK
PASSES = D // K_PASS
GATE_COLS = GATES * H
BANK = 512
HALVES = GATE_COLS // BANK
GATES_PER_HALF = GATES // HALVES
SUBS = 2
BOTH = slice(0, SUBS)
ONE = [slice(r, r + 1) for r in range(SUBS)]
ROUNDS = T // SUBS
WORDS = D // 2
X_BUFS = 6
EARLY = 2
CG_BUFS = 2
GATE_F, GATE_I, GATE_G, GATE_O = range(GATES)
F_SHARE = 32

FLOPS = 2 * T * B * D * GATE_COLS + 2 * B * H * GATE_COLS


def tile_qlstm_t_kernel(tc, inputs, h_0, c_0, W, b, out_0, out_1):
    nc = tc.nc
    hc_steps = out_1.rearrange("a t l n h -> a (t l) n h")

    with ExitStack() as stack:
        const = stack.enter_context(tc.tile_pool(name="const", bufs=1))
        x_pool = stack.enter_context(tc.tile_pool(name="x_pool", bufs=X_BUFS))
        work = stack.enter_context(tc.tile_pool(name="work", bufs=3))
        late = stack.enter_context(tc.tile_pool(name="late", bufs=4))
        psum_t = stack.enter_context(tc.psum_pool(name="psum_t", bufs=2))
        psum_c = stack.enter_context(tc.psum_pool(name="psum_c", bufs=1))
        psum_g = stack.enter_context(tc.psum_pool(name="psum_g", bufs=5))
        stack.enter_context(tc.manual_schedule())

        ident = const.tile([P, P], F32)
        ones = const.tile([P, P], BF16)
        b_row = const.tile([P, GATE_COLS], BF16)
        w_raw = const.tile([P, PASSES * GATES, PACK * H], BF16)
        w_grouped = const.tile([P, PASSES * GATES, H * PACK], BF16, align_bytes=64)
        w_codes = const.tile([P, PASSES, GATE_COLS], U32, align_bytes=256)
        w_scales = const.tile([P, PASSES, GATE_COLS], U8, align_bytes=256)
        wh = const.tile([P, GATES, 2, H], BF16)
        h0_sb = const.tile([P, H], BF16)
        h0_t = const.tile([P, 2, P], BF16)
        c0_sb = const.tile([P, H], BF16)
        ident_bf = const.tile([P, P], BF16)
        c0_ps = psum_c.tile([P, SUBS, H], F32)
        cg_bufs = [const.tile([P, SUBS, F_SHARE + H], F32, name="cg%d" % n) for n in range(CG_BUFS)]
        state_term = const.tile([P, GATE_COLS], F32)
        zero_col = const.tile([P, 1], F32)
        table_warm = const.tile([P, 1], F32)

        x_tiles, xt_tiles, xg_tiles, code_tiles, scale_tiles = {}, {}, {}, {}, {}
        acc_tiles, pre_tiles, act_tiles, fc_ig_tiles, hc_tiles, tanh_c_tiles = {}, {}, {}, {}, {}, {}

        def load_x_tiles(j):
            x_tiles[j] = x_pool.tile([P, SUBS, D], BF16, name="x_sb")
            for r in range(SUBS):
                nc.sync.dma_start(out=x_tiles[j][:, r, :], in_=inputs[j * SUBS + r])

        def load_x(j):
            x_sb = x_pool.tile([P, SUBS, D], BF16)
            if j == 0:
                for r in range(SUBS):
                    nc.sync.dma_start(out=x_sb[:, r, :], in_=inputs[r])
            else:
                nc.sync.dma_start(out=x_sb[:], in_=inputs[j * SUBS : (j + 1) * SUBS].rearrange("r p k -> p r k"))
            x_tiles[j] = x_sb

        def load_w_piece(g, j):
            rows = W[0, j, g * K_PASS : (g + 1) * K_PASS, :]
            nc.sync.dma_start(out=w_raw[:, g * GATES + j, :], in_=rows.rearrange("(q t) c -> q (t c)", t=PACK))

        def load_state_operands():
            nc.sync.dma_start(out=h0_sb[:], in_=h_0[0])
            nc.sync.dma_start(out=c0_sb[:], in_=c_0[0])
            nc.sync.dma_start(out=b_row[0:1, :], in_=b.rearrange("l j c -> l (j c)"))

        def load_wh(half):
            gates = slice(half * GATES_PER_HALF, (half + 1) * GATES_PER_HALF)
            nc.sync.dma_start(
                out=wh[:, gates].rearrange("q j e c -> q j (e c)"),
                in_=W[0, gates, D : D + H, :].rearrange("j (q e) c -> q j (e c)", e=2),
            )

        def regroup_w(engine_copy, g, j):
            piece = g * GATES + j
            engine_copy(
                out=w_grouped[:, piece, :].rearrange("q (c i t) -> q c t i", i=4, t=PACK),
                in_=w_raw[:, piece, :].rearrange("q (t c i) -> q c t i", t=PACK, i=4),
            )

        def quantise_w(g, half):
            cols = slice(half * BANK, (half + 1) * BANK)
            piece = g * GATES + half * GATES_PER_HALF
            nc.vector.quantize_mx(
                out=w_codes[:, g, cols].bitcast(FP8X4),
                scales=w_scales[:, g, cols],
                in_=w_grouped[:, piece : piece + GATES_PER_HALF, :].rearrange("q a n -> q (a n)"),
            )

        def transpose_h0():
            h0_ps = psum_t.tile([P, WORDS // P, P], F32, name="xt")
            nc.tensor.transpose(out=h0_ps[:, 0, :], in_=h0_sb[:].bitcast(F32), identity=ident[:])
            nc.scalar.copy(out=h0_t[:], in_=h0_ps[:, 0, :].bitcast(BF16).rearrange("q (m e) -> q e m", e=2))

        def make_state_term(half, engine_copy):
            cols = slice(half * BANK, (half + 1) * BANK)
            gates = slice(half * GATES_PER_HALF, (half + 1) * GATES_PER_HALF)
            acc = psum_g.tile([P, BANK], F32, name="acc")
            nc.tensor.matmul(out=acc[:], lhsT=ones[:], rhs=b_row[:, cols], start=True, stop=False)
            nc.tensor.matmul(out=acc[:], lhsT=h0_t[:, 0, :], rhs=wh[:, gates, 0, :], start=False, stop=False)
            nc.tensor.matmul(out=acc[:], lhsT=h0_t[:, 1, :], rhs=wh[:, gates, 1, :], start=False, stop=True)
            engine_copy(out=state_term[:, cols], in_=acc[:])

        def transpose_x(j):
            for r in range(SUBS):
                if j < EARLY:
                    xt = psum_g.tile([P, WORDS // P, P], F32, name="acc")
                else:
                    xt = psum_t.tile([P, WORDS // P, P], F32, name="xt")
                x_words = x_tiles[j][:, r, :].bitcast(F32)
                for c in range(WORDS // P):
                    first = c // 2 * 2 * P + c % 2
                    nc.tensor.transpose(
                        out=xt[:, c, :], in_=x_words[:, first : first + 2 * P - 1 : 2], identity=ident[:]
                    )
                xt_tiles[j, r] = xt

        def copy_x(j):
            xg = work.tile([P, SUBS, D], BF16, align_bytes=64)
            for r in range(SUBS):
                nc.scalar.copy(
                    out=xg[:, r, :].bitcast(F32).rearrange("q (g m u) -> q g m u", g=PASSES, u=2),
                    in_=xt_tiles[j, r][:].rearrange("q (g u) m -> q g m u", u=2),
                )
            xg_tiles[j] = xg

        def quantise_x(j):
            x_codes = work.tile([P, SUBS * PASSES * P], U32, align_bytes=256)
            x_scales = work.tile([P, SUBS * PASSES * P], U8, align_bytes=256)
            nc.vector.quantize_mx(
                out=x_codes[:].bitcast(FP8X4),
                scales=x_scales[:],
                in_=xg_tiles[j][:].rearrange("q r n -> q (r n)"),
            )
            code_tiles[j], scale_tiles[j] = x_codes, x_scales

        def half_matmuls(j, half):
            for r in range(SUBS):
                acc = psum_g.tile([P, BANK], F32, name="acc")
                for g in range(PASSES):
                    m_cols = slice((r * PASSES + g) * P, (r * PASSES + g + 1) * P)
                    n_cols = slice(half * BANK, (half + 1) * BANK)
                    nc.tensor.matmul_mx(
                        out=acc[:],
                        lhsT=code_tiles[j][:, m_cols].bitcast(FP8X4),
                        lhsT_scale=scale_tiles[j][:, m_cols],
                        rhs=w_codes[:, g, n_cols].bitcast(FP8X4),
                        rhs_scale=w_scales[:, g, n_cols],
                        start=(g == 0),
                        stop=(g == PASSES - 1),
                    )
                acc_tiles[j, r, half] = acc

        def first_matmuls(j):
            half_matmuls(j, 0)

        def second_matmuls(j):
            half_matmuls(j, 1)

        def add_state(j, half, r):
            if j not in pre_tiles:
                pre_tiles[j] = work.tile([P, SUBS, GATE_COLS], F32, name="pre")
            cols = slice(half * BANK, (half + 1) * BANK)
            nc.vector.tensor_tensor(
                out=pre_tiles[j][:, r, cols], in0=acc_tiles[j, r, half][:], in1=state_term[:, cols], op=ADD
            )

        def add_state_half(j, half):
            for r in range(SUBS):
                add_state(j, half, r)

        def add_first_half(j):
            add_state_half(j, 0)

        def add_second_half(j):
            add_state_half(j, 1)

        def f_and_i(j, rows=BOTH):
            if j not in act_tiles:
                act_tiles[j] = late.tile([P, SUBS, 3 * H], F32, name="act")
            nc.scalar.activation(
                out=act_tiles[j][:, rows, 0 : 2 * H], in_=pre_tiles[j][:, rows, 0 : 2 * H], func=SIGMOID
            )

        def gate_g(j, rows=BOTH):
            nc.scalar.activation(
                out=cg_bufs[j % CG_BUFS][:, rows, F_SHARE:], in_=pre_tiles[j][:, rows, 2 * H : 3 * H], func=TANH
            )

        def gate_o(j, rows=BOTH):
            nc.scalar.activation(
                out=act_tiles[j][:, rows, 2 * H : 3 * H], in_=pre_tiles[j][:, rows, 3 * H : 4 * H], func=SIGMOID
            )

        def g_and_o(j):
            gate_g(j)
            gate_o(j)

        def gate_functions(j):
            f_and_i(j)
            g_and_o(j)

        def i_times_g(j, rows=BOTH, engine=nc.gpsimd):
            if j not in fc_ig_tiles:
                fc_ig_tiles[j] = work.tile([P, SUBS, 2 * H], F32, name="fc_ig")
            engine.tensor_tensor(
                out=fc_ig_tiles[j][:, rows, H - F_SHARE :],
                in0=act_tiles[j][:, rows, H - F_SHARE : 2 * H],
                in1=cg_bufs[j % CG_BUFS][:, rows],
                op=MULT,
            )

        def f_times_c0(j, rows=BOTH):
            own = H - F_SHARE
            nc.vector.tensor_tensor(
                out=fc_ig_tiles[j][:, rows, 0:own], in0=act_tiles[j][:, rows, 0:own], in1=c0_ps[:, rows, 0:own], op=MULT
            )

        def store(dram_steps, j, tile_rows, rows):
            steps = slice(j * SUBS + rows.start, j * SUBS + rows.stop)
            nc.sync.dma_start(out=dram_steps[steps].rearrange("r p h -> p r h"), in_=tile_rows)

        def new_c(j, rows=BOTH):
            if j not in hc_tiles:
                hc_tiles[j] = late.tile([P, 2, SUBS, H], F32, name="hc")
            c = hc_tiles[j][:, 1, rows]
            nc.vector.tensor_tensor(
                out=c, in0=fc_ig_tiles[j][:, rows, 0:H], in1=fc_ig_tiles[j][:, rows, H : 2 * H], op=ADD
            )
            store(hc_steps[1], j, c, rows)

        def tanh_of_c(j, rows=BOTH):
            if j not in tanh_c_tiles:
                tanh_c_tiles[j] = work.tile([P, SUBS, H], F32, name="tanh_c")
            nc.scalar.activation(out=tanh_c_tiles[j][:, rows], in_=hc_tiles[j][:, 1, rows], func=TANH)

        def new_h(j, rows=BOTH, engine=nc.gpsimd):
            h = hc_tiles[j][:, 0, rows]
            engine.tensor_tensor(
                out=h, in0=act_tiles[j][:, rows, 2 * H : 3 * H], in1=tanh_c_tiles[j][:, rows], op=MULT
            )
            store(hc_steps[0], j, h, rows)
            store(out_0, j, h, rows)

        def run(stage, j):
            if 0 <= j < ROUNDS:
                stage(j)

        nc.vector.memset(zero_col[:], 0.0)
        nc.vector.memset(b_row[:].bitcast(U32), 0)
        nc.vector.memset(ones[:], 1.0)
        make_identity(nc, ident[:])
        nc.scalar.activation(out=table_warm[:], in_=zero_col[:], func=SIGMOID)
        vector_copy, scalar_copy = nc.vector.tensor_copy, nc.scalar.copy

        load_w_piece(0, GATE_F)
        load_w_piece(0, GATE_I)
        load_x(0)
        load_w_piece(1, GATE_F)
        load_w_piece(1, GATE_I)
        load_state_operands()
        load_wh(0)
        load_w_piece(0, GATE_G)
        load_w_piece(0, GATE_O)
        load_x(1)
        load_w_piece(1, GATE_G)
        load_w_piece(1, GATE_O)
        load_wh(1)
        load_x_tiles(2)
        for j in range(3, X_BUFS):
            load_x(j)

        regroup_w(vector_copy, 0, GATE_F)
        regroup_w(vector_copy, 0, GATE_I)
        quantise_w(0, 0)
        transpose_x(0)
        load_x(X_BUFS)
        copy_x(0)
        regroup_w(vector_copy, 1, GATE_F)
        regroup_w(vector_copy, 1, GATE_I)
        quantise_w(1, 0)
        quantise_x(0)
        transpose_h0()
        make_state_term(0, scalar_copy)
        nc.vector.tensor_copy(out=ident_bf[:], in_=ident[:])
        for r in range(SUBS):
            nc.tensor.matmul(out=c0_ps[:, r, :], lhsT=ident_bf[:], rhs=c0_sb[:], start=True, stop=True)
        for cg in cg_bufs:
            nc.scalar.copy(
                out=cg[:, :, 0:F_SHARE], in_=c0_sb[:, H - F_SHARE :].unsqueeze(1).to_broadcast([P, SUBS, F_SHARE])
            )
        half_matmuls(0, 0)
        regroup_w(vector_copy, 0, GATE_G)
        regroup_w(vector_copy, 0, GATE_O)
        quantise_w(0, 1)
        transpose_x(1)
        load_x(X_BUFS + 1)
        regroup_w(scalar_copy, 1, GATE_G)
        copy_x(1)
        add_state_half(0, 0)
        regroup_w(vector_copy, 1, GATE_O)
        quantise_w(1, 1)
        make_state_term(1, scalar_copy)
        f_and_i(0)
        quantise_x(1)
        transpose_x(2)
        load_x(X_BUFS + 2)
        half_matmuls(0, 1)
        copy_x(2)
        half_matmuls(1, 0)
        transpose_x(3)
        load_x(X_BUFS + 3)
        half_matmuls(1, 1)
        add_state_half(0, 1)
        g_and_o(0)
        quantise_x(2)

        def step(i):
            run(tanh_of_c, i - 2)
            run(copy_x, i + 2)
            run(first_matmuls, i + 1)
            run(transpose_x, i + 3)
            run(second_matmuls, i + 1)
            run(i_times_g, i - 1)
            run(new_h, i - 2)
            run(add_first_half, i)
            run(f_times_c0, i - 1)
            run(add_second_half, i)
            run(gate_functions, i)
            run(quantise_x, i + 2)
            run(new_c, i - 1)
            run(load_x, i + 3 + X_BUFS)

        for i in range(1, ROUNDS - 2):
            step(i)

        last = ROUNDS - 1
        prev = last - 1
        tanh_of_c(prev - 2)
        first_matmuls(last)
        second_matmuls(last)
        i_times_g(prev - 1)
        new_h(prev - 2)
        add_first_half(prev)
        f_times_c0(prev - 1)
        add_second_half(prev)
        f_and_i(prev)
        gate_g(prev)
        new_c(prev - 1)
        tanh_of_c(prev - 1)
        gate_o(prev)
        i_times_g(prev, ONE[0])
        new_h(prev - 1)
        f_times_c0(prev)
        for r in range(SUBS):
            add_state(last, 0, r)
            add_state(last, 1, r)
            f_and_i(last, ONE[r])
            gate_g(last, ONE[r])
        new_c(prev, ONE[0])
        tanh_of_c(prev, ONE[0])
        i_times_g(prev, ONE[1], nc.vector)
        new_c(prev, ONE[1])
        tanh_of_c(prev, ONE[1])
        gate_o(last)
        for r in range(SUBS):
            i_times_g(last, ONE[r], nc.vector)
            f_times_c0(last, ONE[r])
            new_h(prev, ONE[r], nc.vector)
            new_c(last, ONE[r])
            tanh_of_c(last, ONE[r])
        for r in range(SUBS):
            new_h(last, ONE[r], nc.vector)
